import numpy as np
import ml_dtypes


def mxq(x, axis, fmt="e4m3"):
    dtype, down = {"e4m3": (ml_dtypes.float8_e4m3fn, 7), "e5m2": (ml_dtypes.float8_e5m2, 14)}[fmt]
    v = np.moveaxis(np.asarray(x, np.float32).astype(ml_dtypes.bfloat16).astype(np.float64), axis, -1)
    blocks = v.reshape(v.shape[:-1] + (-1, 32))
    amax = np.abs(blocks).max(-1, keepdims=True)
    byte = np.maximum(np.where(amax > 0, np.frexp(amax)[1] - 1 + 127, 0) - down, 1)
    scale = np.exp2(byte - 127.0)
    codes = (blocks / scale).astype(np.float32).astype(dtype).astype(np.float64)
    return np.moveaxis((codes * scale).reshape(v.shape), -1, axis)


WIDE = False


def mx_kscale(k):
    if not WIDE:
        return np.ones(k)
    levels = np.array([10, -10, 5, -5, 0])
    a = np.random.permutation(np.resize(levels, k // 512 * 4)).reshape(k // 512, 4)
    idx = np.arange(k)
    return np.exp2(a[idx // 512, idx % 128 // 32])


BF16 = ml_dtypes.bfloat16


def bf(x):
    return np.asarray(x, np.float32).astype(BF16)


def f64(x):
    return np.asarray(x).astype(np.float64)


E2M1 = np.array([0.0, 0.5, 1.0, 1.5, 2.0, 3.0, 4.0, 6.0, -0.0, -0.5, -1.0, -1.5, -2.0, -3.0, -4.0, -6.0])


def pack_weight(w, fmt):
    k, n = w.shape
    w = f64(bf(w)).reshape(k // 32, 32, n)
    amax = np.abs(w).max(1)
    if fmt == "e4m3":
        byte = np.frexp(amax)[1] - 1 + 127 - 7
    else:
        mant, ex = np.frexp(amax / 6.0)
        byte = np.where(mant > 0.5, ex, ex - 1) + 127
    byte = np.clip(np.where(amax > 0, byte, 1), 1, 254)
    scaled = (w * np.exp2(127.0 - byte)[:, None, :]).reshape(k, n).astype(np.float32)
    by_word = np.ascontiguousarray(scaled.reshape(k // 512, 128, 4, n).transpose(0, 1, 3, 2))
    if fmt == "e4m3":
        words = by_word.astype(ml_dtypes.float8_e4m3fn).view(np.uint8)
    else:
        c = by_word.astype(ml_dtypes.float4_e2m1fn).view(np.uint8) & 0xF
        words = c[..., 0::2] | (c[..., 1::2] << 4)
    return np.ascontiguousarray(words), np.ascontiguousarray(byte.astype(np.uint8).reshape(k // 512, 16, n))


def unpack_weight(words, scales, fmt):
    g, p, n, _ = words.shape
    if fmt == "e4m3":
        vals = np.ascontiguousarray(words).view(ml_dtypes.float8_e4m3fn).astype(np.float64)
    else:
        nib = np.empty((g, p, n, 4), np.uint8)
        nib[..., 0::2] = words & 0xF
        nib[..., 1::2] = words >> 4
        vals = E2M1[nib]
    vals = vals * np.repeat(np.exp2(scales.astype(np.float64) - 127.0), 8, axis=1)[..., None]
    return vals.transpose(0, 1, 3, 2).reshape(g * 512, n)

def pack4(w):
    words, scales = pack_weight(w, "e2m1")
    return words.reshape(words.shape[0], 128, -1), scales


def unpack4(words, scales):
    return unpack_weight(words.reshape(words.shape[0], 128, -1, 2), scales, "e2m1")


N1, N2, N3, R1, R = 128, 128, 128, 512, 1024


def setup_inputs():
    s = mx_kscale(R)
    g = R ** (-1.0 / 6.0)
    X = bf(np.random.standard_normal((N1, N2, N3)))
    A = bf(np.random.standard_normal((N1, R)) * g * s)
    B = bf(np.random.standard_normal((N2, R)) * g)
    c = np.random.standard_normal((N3, R)) * g / s
    words, scales = pack4(np.ascontiguousarray(c.T))
    return {"X": X, "A": A, "B": B, "C_words": words, "C_scales": scales}


def reference(X, A, B, C_words, C_scales):
    p = (f64(A)[:, None, :] * f64(B)[None, :, :]).reshape(N1 * N2, R)
    approx = mxq(p, 1, "e4m3") @ unpack4(C_words, C_scales)
    return approx.reshape(N1, N2, N3) - f64(X)

@@ -1,0 +1,170 @@
+from contextlib import ExitStack
+
+import concourse.mybir as mybir
+from concourse.masks import make_identity
+
+F32 = mybir.dt.float32
+BF16 = mybir.dt.bfloat16
+I32 = mybir.dt.int32
+U32 = mybir.dt.uint32
+U8 = mybir.dt.uint8
+FP8X4 = mybir.dt.float8_e4m3fn_x4
+FP4X4 = mybir.dt.float4_e2m1fn_x4
+
+P = 128
+PACK = 4
+N1, N2, N3, R = 128, 128, 128, 1024
+PASSES = R // (P * PACK)
+WORDS = R // 2
+HALVES = PACK // 2
+
+J_BLOCK = 4
+N_BLOCKS = N2 // J_BLOCK
+SCALAR_EVERY = 3
+SUBTRACT_LAG = 3
+X_CHUNK = 16
+
+FLOPS = 2 * N1 * N2 * N3 * R
+
+
+def tile_recon_loss_pa_t_kernel(tc, X, A, B, C_words, C_scales, out):
+    nc = tc.nc
+    block_shape = [P, J_BLOCK, PASSES, N1, PACK]
+
+    with ExitStack() as stack:
+        stack.enter_context(tc.manual_schedule())
+        keep = stack.enter_context(tc.tile_pool(name="keep", bufs=1))
+        vector_products = stack.enter_context(tc.tile_pool(name="vector_products", bufs=3))
+        scalar_products = stack.enter_context(tc.tile_pool(name="scalar_products", bufs=2))
+        quantised = stack.enter_context(tc.tile_pool(name="quantised", bufs=3))
+        results = stack.enter_context(tc.tile_pool(name="results", bufs=4))
+        turned = stack.enter_context(tc.psum_pool(name="turned", bufs=1))
+        sums = stack.enter_context(tc.psum_pool(name="sums", bufs=4))
+
+        w_scales = keep.tile([P, PASSES, N3], U8, align_bytes=64)
+        nc.vector.memset(w_scales[:].bitcast(I32), 0)
+
+        a_rows = keep.tile([N1, R], BF16)
+        b_rows = keep.tile([N2, R], BF16)
+        nc.sync.dma_start(out=b_rows[:], in_=B)
+        nc.scalar.dma_start(out=a_rows[:], in_=A)
+
+        w_words = keep.tile([P, PASSES, 2 * N3], U8, align_bytes=64)
+        nc.sync.dma_start(
+            out=w_words[:].bitcast(I32), in_=C_words.bitcast(I32).rearrange("g p w -> p g w")
+        )
+        for quadrant in range(4):
+            nc.sync.dma_start(
+                out=w_scales[32 * quadrant : 32 * quadrant + 4].bitcast(I32),
+                in_=C_scales.bitcast(I32)[:, 4 * quadrant : 4 * quadrant + 4, :].rearrange(
+                    "g q w -> q g w"
+                ),
+            )
+
+        x_chunks = []
+        for c in range(N2 // X_CHUNK):
+            x_chunk = keep.tile([N1, X_CHUNK, N3], BF16, name="x_chunk%d" % c)
+            nc.sync.dma_start(out=x_chunk[:], in_=X[:, c * X_CHUNK : (c + 1) * X_CHUNK, :])
+            x_chunks.append(x_chunk)
+
+        identity = keep.tile([P, P], F32)
+        make_identity(nc, identity[:])
+        b_turned = turned.tile([P, PASSES, HALVES, N2], F32)
+        a_turned = turned.tile([P, PASSES, HALVES, N1], F32)
+        for rows, rows_turned in ((b_rows, b_turned), (a_rows, a_turned)):
+            for g in range(PASSES):
+                for h in range(HALVES):
+                    first = g * (WORDS // PASSES) + h
+                    nc.tensor.transpose(
+                        rows_turned[:, g, h, :],
+                        rows[:].bitcast(F32)[:, first : (g + 1) * (WORDS // PASSES) : HALVES],
+                        identity[:],
+                    )
+        bt = keep.tile([P, N2, PASSES, PACK], BF16)
+        at = keep.tile([P, PASSES, N1, PACK], BF16)
+        nc.vector.tensor_copy(out=bt[:].bitcast(F32), in_=b_turned[:].rearrange("p g h j -> p j g h"))
+        nc.scalar.copy(out=at[:].bitcast(F32), in_=a_turned[:].rearrange("p g h i -> p g i h"))
+        bt_f32 = keep.tile([P, N2, PASSES, PACK], F32)
+        nc.scalar.copy(out=bt_f32[:], in_=bt[:])
+
+        def multiply_on_vector(j0):
+            product = vector_products.tile(block_shape, BF16, align_bytes=64, name="vector_product")
+            nc.vector.tensor_tensor(
+                out=product[:],
+                in0=bt[:, j0 : j0 + J_BLOCK, :, :].unsqueeze(3).to_broadcast(block_shape),
+                in1=at[:].unsqueeze(1).to_broadcast(block_shape),
+                op=mybir.AluOpType.mult,
+            )
+            return product
+
+        def multiply_on_scalar(j0):
+            planes = scalar_products.tile([P, J_BLOCK, PASSES, PACK, N1], BF16, name="planes")
+            product = scalar_products.tile(block_shape, BF16, align_bytes=64, name="scalar_product")
+
+            def group_planes(jl, g):
+                nc.scalar.copy(
+                    out=product[:, jl, g, :, :].rearrange("p (c i) t -> p c t i", i=4),
+                    in_=planes[:, jl, g, :, :].rearrange("p t (c i) -> p c t i", i=4),
+                )
+
+            pairs = [(jl, g) for jl in range(J_BLOCK) for g in range(PASSES)]
+            for n, (jl, g) in enumerate(pairs):
+                for t in range(PACK):
+                    nc.scalar.activation(
+                        out=planes[:, jl, g, t, :],
+                        in_=at[:, g, :, t],
+                        func=mybir.ActivationFunctionType.Copy,
+                        scale=bt_f32[:, j0 + jl, g, t : t + 1],
+                    )
+                if n > 0:
+                    group_planes(*pairs[n - 1])
+            group_planes(*pairs[-1])
+            return product
+
+        def quantise_and_contract(product):
+            codes = quantised.tile([P, J_BLOCK * PASSES * N1], U32, align_bytes=64, name="codes")
+            scales = quantised.tile([P, J_BLOCK * PASSES * N1], U8, align_bytes=64, name="scales")
+            nc.vector.quantize_mx(
+                out=codes[:].bitcast(FP8X4),
+                scales=scales[:],
+                in_=product[:].rearrange("p j g i t -> p (j g i t)"),
+            )
+            acc = sums.tile([P, J_BLOCK, N3], F32, name="acc")
+            for jl in range(J_BLOCK):
+                for g in range(PASSES):
+                    first = (jl * PASSES + g) * N1
+                    nc.tensor.matmul_mx(
+                        out=acc[:, jl, :],
+                        lhsT=codes[:, first : first + N1].bitcast(FP8X4),
+                        lhsT_scale=scales[:, first : first + N1],
+                        rhs=w_words[:, g, :].bitcast(FP4X4),
+                        rhs_scale=w_scales[:, g, :],
+                        start=(g == 0),
+                        stop=(g == PASSES - 1),
+                    )
+            return acc
+
+        def subtract_and_store(j0, acc):
+            x_chunk = x_chunks[j0 // X_CHUNK]
+            first = j0 % X_CHUNK
+            result = results.tile([P, J_BLOCK, N3], F32, name="result")
+            nc.vector.tensor_tensor(
+                out=result[:],
+                in0=acc[:],
+                in1=x_chunk[:, first : first + J_BLOCK, :],
+                op=mybir.AluOpType.subtract,
+            )
+            nc.sync.dma_start(out=out[:, j0 : j0 + J_BLOCK, :], in_=result[:])
+
+        products = {}
+        accs = {}
+        for step in range(N_BLOCKS + SUBTRACT_LAG):
+            if step < N_BLOCKS:
+                if step % SCALAR_EVERY == SCALAR_EVERY - 1:
+                    products[step] = multiply_on_scalar(step * J_BLOCK)
+                else:
+                    products[step] = multiply_on_vector(step * J_BLOCK)
+            if 1 <= step <= N_BLOCKS:
+                accs[step - 1] = quantise_and_contract(products[step - 1])
+            if step >= SUBTRACT_LAG:
+                subtract_and_store((step - SUBTRACT_LAG) * J_BLOCK, accs[step - SUBTRACT_LAG])

@@ -18,28 +18,28 @@ PASSES = R // (P * PACK)
 WORDS = R // 2
 HALVES = PACK // 2
 
-J_BLOCK = 4
-N_BLOCKS = N2 // J_BLOCK
-SCALAR_EVERY = 3
-SUBTRACT_LAG = 3
-X_CHUNK = 16
+J_GROUP = 4
+J_STEP = 16
+GROUPS = J_STEP // J_GROUP
+N_STEPS = N2 // J_STEP
+J_VECTOR = 9
+J_GPSIMD = 2
+J_SCALAR = J_STEP - J_VECTOR - J_GPSIMD
 
 FLOPS = 2 * N1 * N2 * N3 * R
 
 
 def tile_recon_loss_pa_t_kernel(tc, X, A, B, C_words, C_scales, out):
     nc = tc.nc
-    block_shape = [P, J_BLOCK, PASSES, N1, PACK]
 
     with ExitStack() as stack:
         stack.enter_context(tc.manual_schedule())
         keep = stack.enter_context(tc.tile_pool(name="keep", bufs=1))
-        vector_products = stack.enter_context(tc.tile_pool(name="vector_products", bufs=3))
-        scalar_products = stack.enter_context(tc.tile_pool(name="scalar_products", bufs=2))
-        quantised = stack.enter_context(tc.tile_pool(name="quantised", bufs=3))
-        results = stack.enter_context(tc.tile_pool(name="results", bufs=4))
+        products = stack.enter_context(tc.tile_pool(name="products", bufs=2))
+        quantised = stack.enter_context(tc.tile_pool(name="quantised", bufs=GROUPS + 1))
+        results = stack.enter_context(tc.tile_pool(name="results", bufs=GROUPS + 2))
         turned = stack.enter_context(tc.psum_pool(name="turned", bufs=1))
-        sums = stack.enter_context(tc.psum_pool(name="sums", bufs=4))
+        sums = stack.enter_context(tc.psum_pool(name="sums", bufs=GROUPS))
 
         w_scales = keep.tile([P, PASSES, N3], U8, align_bytes=64)
         nc.vector.memset(w_scales[:].bitcast(I32), 0)
@@ -61,110 +61,111 @@ def tile_recon_loss_pa_t_kernel(tc, X, A, B, C_words, C_scales, out):
                 ),
             )
 
-        x_chunks = []
-        for c in range(N2 // X_CHUNK):
-            x_chunk = keep.tile([N1, X_CHUNK, N3], BF16, name="x_chunk%d" % c)
-            nc.sync.dma_start(out=x_chunk[:], in_=X[:, c * X_CHUNK : (c + 1) * X_CHUNK, :])
-            x_chunks.append(x_chunk)
+        x_steps = []
+        for step in range(N_STEPS):
+            x_step = keep.tile([N1, J_STEP, N3], BF16, name="x_step%d" % step)
+            nc.sync.dma_start(out=x_step[:], in_=X[:, step * J_STEP : (step + 1) * J_STEP, :])
+            x_steps.append(x_step)
 
         identity = keep.tile([P, P], F32)
         make_identity(nc, identity[:])
-        b_turned = turned.tile([P, PASSES, HALVES, N2], F32)
-        a_turned = turned.tile([P, PASSES, HALVES, N1], F32)
-        for rows, rows_turned in ((b_rows, b_turned), (a_rows, a_turned)):
-            for g in range(PASSES):
-                for h in range(HALVES):
-                    first = g * (WORDS // PASSES) + h
-                    nc.tensor.transpose(
-                        rows_turned[:, g, h, :],
-                        rows[:].bitcast(F32)[:, first : (g + 1) * (WORDS // PASSES) : HALVES],
-                        identity[:],
-                    )
+        b_turned = turned.tile([P, N2, PASSES, HALVES], F32)
+        a_turned = turned.tile([P, PASSES, N1, HALVES], F32)
+        for g in range(PASSES):
+            for h in range(HALVES):
+                columns = slice(g * (WORDS // PASSES) + h, (g + 1) * (WORDS // PASSES), HALVES)
+                nc.tensor.transpose(b_turned[:, :, g, h], b_rows[:].bitcast(F32)[:, columns], identity[:])
+        for g in range(PASSES):
+            for h in range(HALVES):
+                columns = slice(g * (WORDS // PASSES) + h, (g + 1) * (WORDS // PASSES), HALVES)
+                nc.tensor.transpose(a_turned[:, g, :, h], a_rows[:].bitcast(F32)[:, columns], identity[:])
         bt = keep.tile([P, N2, PASSES, PACK], BF16)
         at = keep.tile([P, PASSES, N1, PACK], BF16)
-        nc.vector.tensor_copy(out=bt[:].bitcast(F32), in_=b_turned[:].rearrange("p g h j -> p j g h"))
-        nc.scalar.copy(out=at[:].bitcast(F32), in_=a_turned[:].rearrange("p g h i -> p g i h"))
+        nc.vector.tensor_copy(out=bt[:].bitcast(F32), in_=b_turned[:])
+        nc.vector.tensor_copy(out=at[:].bitcast(F32), in_=a_turned[:])
+        at_in_psum = a_turned[:].bitcast(BF16)
         bt_f32 = keep.tile([P, N2, PASSES, PACK], F32)
         nc.scalar.copy(out=bt_f32[:], in_=bt[:])
 
-        def multiply_on_vector(j0):
-            product = vector_products.tile(block_shape, BF16, align_bytes=64, name="vector_product")
-            nc.vector.tensor_tensor(
-                out=product[:],
-                in0=bt[:, j0 : j0 + J_BLOCK, :, :].unsqueeze(3).to_broadcast(block_shape),
-                in1=at[:].unsqueeze(1).to_broadcast(block_shape),
+        def multiply_by_tensor_tensor(engine, a_factor, product, first, count, j0):
+            shape = [P, count, PASSES, N1, PACK]
+            engine.tensor_tensor(
+                out=product[:, first : first + count],
+                in0=bt[:, j0 + first : j0 + first + count].unsqueeze(3).to_broadcast(shape),
+                in1=a_factor.unsqueeze(1).to_broadcast(shape),
                 op=mybir.AluOpType.mult,
             )
-            return product
 
-        def multiply_on_scalar(j0):
-            planes = scalar_products.tile([P, J_BLOCK, PASSES, PACK, N1], BF16, name="planes")
-            product = scalar_products.tile(block_shape, BF16, align_bytes=64, name="scalar_product")
+        def multiply_on_scalar(product, first, count, j0):
+            planes = products.tile([P, count, PASSES, PACK, N1], BF16, name="planes")
 
             def group_planes(jl, g):
                 nc.scalar.copy(
-                    out=product[:, jl, g, :, :].rearrange("p (c i) t -> p c t i", i=4),
+                    out=product[:, first + jl, g, :, :].rearrange("p (c i) t -> p c t i", i=4),
                     in_=planes[:, jl, g, :, :].rearrange("p t (c i) -> p c t i", i=4),
                 )
 
-            pairs = [(jl, g) for jl in range(J_BLOCK) for g in range(PASSES)]
+            pairs = [(jl, g) for jl in range(count) for g in range(PASSES)]
             for n, (jl, g) in enumerate(pairs):
                 for t in range(PACK):
                     nc.scalar.activation(
                         out=planes[:, jl, g, t, :],
                         in_=at[:, g, :, t],
                         func=mybir.ActivationFunctionType.Copy,
-                        scale=bt_f32[:, j0 + jl, g, t : t + 1],
+                        scale=bt_f32[:, j0 + first + jl, g, t : t + 1],
                     )
                 if n > 0:
                     group_planes(*pairs[n - 1])
             group_planes(*pairs[-1])
+
+        def multiply(j0):
+            product = products.tile([P, J_STEP, PASSES, N1, PACK], BF16, align_bytes=64, name="product")
+            multiply_by_tensor_tensor(nc.vector, at_in_psum, product, 0, J_VECTOR, j0)
+            multiply_by_tensor_tensor(nc.gpsimd, at[:], product, J_VECTOR, J_GPSIMD, j0)
+            multiply_on_scalar(product, J_VECTOR + J_GPSIMD, J_SCALAR, j0)
             return product
 
         def quantise_and_contract(product):
-            codes = quantised.tile([P, J_BLOCK * PASSES * N1], U32, align_bytes=64, name="codes")
-            scales = quantised.tile([P, J_BLOCK * PASSES * N1], U8, align_bytes=64, name="scales")
-            nc.vector.quantize_mx(
-                out=codes[:].bitcast(FP8X4),
-                scales=scales[:],
-                in_=product[:].rearrange("p j g i t -> p (j g i t)"),
-            )
-            acc = sums.tile([P, J_BLOCK, N3], F32, name="acc")
-            for jl in range(J_BLOCK):
-                for g in range(PASSES):
-                    first = (jl * PASSES + g) * N1
-                    nc.tensor.matmul_mx(
-                        out=acc[:, jl, :],
-                        lhsT=codes[:, first : first + N1].bitcast(FP8X4),
-                        lhsT_scale=scales[:, first : first + N1],
-                        rhs=w_words[:, g, :].bitcast(FP4X4),
-                        rhs_scale=w_scales[:, g, :],
-                        start=(g == 0),
-                        stop=(g == PASSES - 1),
-                    )
-            return acc
+            accs = []
+            for group in range(GROUPS):
+                codes = quantised.tile([P, J_GROUP * PASSES * N1], U32, align_bytes=64, name="codes")
+                scales = quantised.tile([P, J_GROUP * PASSES * N1], U8, align_bytes=64, name="scales")
+                nc.vector.quantize_mx(
+                    out=codes[:].bitcast(FP8X4),
+                    scales=scales[:],
+                    in_=product[:, group * J_GROUP : (group + 1) * J_GROUP].rearrange(
+                        "p j g i t -> p (j g i t)"
+                    ),
+                )
+                acc = sums.tile([P, J_GROUP, N3], F32, name="acc")
+                for jl in range(J_GROUP):
+                    for g in range(PASSES):
+                        first = (jl * PASSES + g) * N1
+                        nc.tensor.matmul_mx(
+                            out=acc[:, jl, :],
+                            lhsT=codes[:, first : first + N1].bitcast(FP8X4),
+                            lhsT_scale=scales[:, first : first + N1],
+                            rhs=w_words[:, g, :].bitcast(FP4X4),
+                            rhs_scale=w_scales[:, g, :],
+                            start=(g == 0),
+                            stop=(g == PASSES - 1),
+                        )
+                accs.append(acc)
+            return accs
 
-        def subtract_and_store(j0, acc):
-            x_chunk = x_chunks[j0 // X_CHUNK]
-            first = j0 % X_CHUNK
-            result = results.tile([P, J_BLOCK, N3], F32, name="result")
-            nc.vector.tensor_tensor(
-                out=result[:],
-                in0=acc[:],
-                in1=x_chunk[:, first : first + J_BLOCK, :],
-                op=mybir.AluOpType.subtract,
-            )
-            nc.sync.dma_start(out=out[:, j0 : j0 + J_BLOCK, :], in_=result[:])
+        def subtract_and_store(step, accs):
+            for group in range(GROUPS):
+                js = slice(group * J_GROUP, (group + 1) * J_GROUP)
+                result = results.tile([P, J_GROUP, N3], F32, name="result")
+                nc.vector.tensor_tensor(
+                    out=result[:], in0=accs[group][:], in1=x_steps[step][:, js, :], op=mybir.AluOpType.subtract
+                )
+                first = step * J_STEP + group * J_GROUP
+                nc.sync.dma_start(out=out[:, first : first + J_GROUP, :], in_=result[:])
 
-        products = {}
-        accs = {}
-        for step in range(N_BLOCKS + SUBTRACT_LAG):
-            if step < N_BLOCKS:
-                if step % SCALAR_EVERY == SCALAR_EVERY - 1:
-                    products[step] = multiply_on_scalar(step * J_BLOCK)
-                else:
-                    products[step] = multiply_on_vector(step * J_BLOCK)
-            if 1 <= step <= N_BLOCKS:
-                accs[step - 1] = quantise_and_contract(products[step - 1])
-            if step >= SUBTRACT_LAG:
-                subtract_and_store((step - SUBTRACT_LAG) * J_BLOCK, accs[step - SUBTRACT_LAG])
+        step_products = {}
+        for step in range(N_STEPS + 1):
+            if step < N_STEPS:
+                step_products[step] = multiply(step * J_STEP)
+            if step >= 1:
+                subtract_and_store(step - 1, quantise_and_contract(step_products[step - 1]))

@@ -22,9 +22,10 @@ J_GROUP = 4
 J_STEP = 16
 GROUPS = J_STEP // J_GROUP
 N_STEPS = N2 // J_STEP
-J_VECTOR = 9
-J_GPSIMD = 2
-J_SCALAR = J_STEP - J_VECTOR - J_GPSIMD
+PAIRS_STEP = J_STEP * PASSES
+PAIRS_VECTOR = 18
+PAIRS_GPSIMD = 5
+PAIRS_SCALAR = PAIRS_STEP - PAIRS_VECTOR - PAIRS_GPSIMD
 
 FLOPS = 2 * N1 * N2 * N3 * R
 
@@ -87,42 +88,51 @@ def tile_recon_loss_pa_t_kernel(tc, X, A, B, C_words, C_scales, out):
         bt_f32 = keep.tile([P, N2, PASSES, PACK], F32)
         nc.scalar.copy(out=bt_f32[:], in_=bt[:])
 
-        def multiply_by_tensor_tensor(engine, a_factor, product, first, count, j0):
-            shape = [P, count, PASSES, N1, PACK]
+        def multiply_by_tensor_tensor(engine, a_factor, product, j0, first, count):
+            jl, whole = first // PASSES, count // PASSES
+            shape = [P, whole, PASSES, N1, PACK]
             engine.tensor_tensor(
-                out=product[:, first : first + count],
-                in0=bt[:, j0 + first : j0 + first + count].unsqueeze(3).to_broadcast(shape),
+                out=product[:, jl : jl + whole],
+                in0=bt[:, j0 + jl : j0 + jl + whole].unsqueeze(3).to_broadcast(shape),
                 in1=a_factor.unsqueeze(1).to_broadcast(shape),
                 op=mybir.AluOpType.mult,
             )
-
-        def multiply_on_scalar(product, first, count, j0):
-            planes = products.tile([P, count, PASSES, PACK, N1], BF16, name="planes")
-
-            def group_planes(jl, g):
-                nc.scalar.copy(
-                    out=product[:, first + jl, g, :, :].rearrange("p (c i) t -> p c t i", i=4),
-                    in_=planes[:, jl, g, :, :].rearrange("p t (c i) -> p c t i", i=4),
+            if count % PASSES:
+                engine.tensor_tensor(
+                    out=product[:, jl + whole, 0],
+                    in0=bt[:, j0 + jl + whole, 0].unsqueeze(1).to_broadcast([P, N1, PACK]),
+                    in1=a_factor[:, 0],
+                    op=mybir.AluOpType.mult,
                 )
 
-            pairs = [(jl, g) for jl in range(count) for g in range(PASSES)]
-            for n, (jl, g) in enumerate(pairs):
+        def multiply_on_scalar(product, j0, first, count):
+            planes = products.tile([P, count, PACK, N1], BF16, name="planes")
+
+            def group_planes(n):
+                pair = first + n
+                nc.scalar.copy(
+                    out=product[:, pair // PASSES, pair % PASSES].rearrange("p (c i) t -> p c t i", i=4),
+                    in_=planes[:, n].rearrange("p t (c i) -> p c t i", i=4),
+                )
+
+            for n in range(count):
+                pair = first + n
                 for t in range(PACK):
                     nc.scalar.activation(
-                        out=planes[:, jl, g, t, :],
-                        in_=at[:, g, :, t],
+                        out=planes[:, n, t, :],
+                        in_=at[:, pair % PASSES, :, t],
                         func=mybir.ActivationFunctionType.Copy,
-                        scale=bt_f32[:, j0 + first + jl, g, t : t + 1],
+                        scale=bt_f32[:, j0 + pair // PASSES, pair % PASSES, t : t + 1],
                     )
                 if n > 0:
-                    group_planes(*pairs[n - 1])
-            group_planes(*pairs[-1])
+                    group_planes(n - 1)
+            group_planes(count - 1)
 
         def multiply(j0):
             product = products.tile([P, J_STEP, PASSES, N1, PACK], BF16, align_bytes=64, name="product")
-            multiply_by_tensor_tensor(nc.vector, at_in_psum, product, 0, J_VECTOR, j0)
-            multiply_by_tensor_tensor(nc.gpsimd, at[:], product, J_VECTOR, J_GPSIMD, j0)
-            multiply_on_scalar(product, J_VECTOR + J_GPSIMD, J_SCALAR, j0)
+            multiply_by_tensor_tensor(nc.vector, at_in_psum, product, j0, 0, PAIRS_VECTOR)
+            multiply_by_tensor_tensor(nc.gpsimd, at[:], product, j0, PAIRS_VECTOR, PAIRS_GPSIMD)
+            multiply_on_scalar(product, j0, PAIRS_VECTOR + PAIRS_GPSIMD, PAIRS_SCALAR)
             return product
 
         def quantise_and_contract(product):

@@ -23,8 +23,8 @@ J_STEP = 16
 GROUPS = J_STEP // J_GROUP
 N_STEPS = N2 // J_STEP
 PAIRS_STEP = J_STEP * PASSES
-PAIRS_VECTOR = 18
-PAIRS_GPSIMD = 5
+PAIRS_VECTOR = 17
+PAIRS_GPSIMD = 6
 PAIRS_SCALAR = PAIRS_STEP - PAIRS_VECTOR - PAIRS_GPSIMD
 
 FLOPS = 2 * N1 * N2 * N3 * R
@@ -89,21 +89,30 @@ def tile_recon_loss_pa_t_kernel(tc, X, A, B, C_words, C_scales, out):
         nc.scalar.copy(out=bt_f32[:], in_=bt[:])
 
         def multiply_by_tensor_tensor(engine, a_factor, product, j0, first, count):
-            jl, whole = first // PASSES, count // PASSES
-            shape = [P, whole, PASSES, N1, PACK]
-            engine.tensor_tensor(
-                out=product[:, jl : jl + whole],
-                in0=bt[:, j0 + jl : j0 + jl + whole].unsqueeze(3).to_broadcast(shape),
-                in1=a_factor.unsqueeze(1).to_broadcast(shape),
-                op=mybir.AluOpType.mult,
-            )
-            if count % PASSES:
+            def one_pair(pair):
+                jl, g = pair // PASSES, pair % PASSES
                 engine.tensor_tensor(
-                    out=product[:, jl + whole, 0],
-                    in0=bt[:, j0 + jl + whole, 0].unsqueeze(1).to_broadcast([P, N1, PACK]),
-                    in1=a_factor[:, 0],
+                    out=product[:, jl, g],
+                    in0=bt[:, j0 + jl, g].unsqueeze(1).to_broadcast([P, N1, PACK]),
+                    in1=a_factor[:, g],
                     op=mybir.AluOpType.mult,
                 )
+
+            last = first + count
+            if first % PASSES:
+                one_pair(first)
+                first += 1
+            jl, whole = first // PASSES, (last - first) // PASSES
+            if whole:
+                shape = [P, whole, PASSES, N1, PACK]
+                engine.tensor_tensor(
+                    out=product[:, jl : jl + whole],
+                    in0=bt[:, j0 + jl : j0 + jl + whole].unsqueeze(3).to_broadcast(shape),
+                    in1=a_factor.unsqueeze(1).to_broadcast(shape),
+                    op=mybir.AluOpType.mult,
+                )
+            if (last - first) % PASSES:
+                one_pair(last - 1)
 
         def multiply_on_scalar(product, j0, first, count):
             planes = products.tile([P, count, PACK, N1], BF16, name="planes")

@@ -140,8 +140,8 @@ def tile_recon_loss_pa_t_kernel(tc, X, A, B, C_words, C_scales, out):
         def multiply(j0):
             product = products.tile([P, J_STEP, PASSES, N1, PACK], BF16, align_bytes=64, name="product")
             multiply_by_tensor_tensor(nc.vector, at_in_psum, product, j0, 0, PAIRS_VECTOR)
-            multiply_by_tensor_tensor(nc.gpsimd, at[:], product, j0, PAIRS_VECTOR, PAIRS_GPSIMD)
-            multiply_on_scalar(product, j0, PAIRS_VECTOR + PAIRS_GPSIMD, PAIRS_SCALAR)
+            multiply_by_tensor_tensor(nc.gpsimd, at[:], product, j0, PAIRS_STEP - PAIRS_GPSIMD, PAIRS_GPSIMD)
+            multiply_on_scalar(product, j0, PAIRS_VECTOR, PAIRS_SCALAR)
             return product
 
         def quantise_and_contract(product):

@@ -23,9 +23,14 @@ J_STEP = 16
 GROUPS = J_STEP // J_GROUP
 N_STEPS = N2 // J_STEP
 PAIRS_STEP = J_STEP * PASSES
-PAIRS_VECTOR = 17
-PAIRS_GPSIMD = 6
-PAIRS_SCALAR = PAIRS_STEP - PAIRS_VECTOR - PAIRS_GPSIMD
+
+
+def shares(step):
+    if step < 2:
+        vector, gpsimd = 19, 4
+    else:
+        vector, gpsimd = 18, 5
+    return vector, PAIRS_STEP - vector - gpsimd, gpsimd
 
 FLOPS = 2 * N1 * N2 * N3 * R
 
@@ -137,11 +142,13 @@ def tile_recon_loss_pa_t_kernel(tc, X, A, B, C_words, C_scales, out):
                     group_planes(n - 1)
             group_planes(count - 1)
 
-        def multiply(j0):
+        def multiply(step):
+            j0 = step * J_STEP
+            pairs_vector, pairs_scalar, pairs_gpsimd = shares(step)
             product = products.tile([P, J_STEP, PASSES, N1, PACK], BF16, align_bytes=64, name="product")
-            multiply_by_tensor_tensor(nc.vector, at_in_psum, product, j0, 0, PAIRS_VECTOR)
-            multiply_by_tensor_tensor(nc.gpsimd, at[:], product, j0, PAIRS_STEP - PAIRS_GPSIMD, PAIRS_GPSIMD)
-            multiply_on_scalar(product, j0, PAIRS_VECTOR, PAIRS_SCALAR)
+            multiply_by_tensor_tensor(nc.vector, at_in_psum, product, j0, 0, pairs_vector)
+            multiply_by_tensor_tensor(nc.gpsimd, at[:], product, j0, PAIRS_STEP - pairs_gpsimd, pairs_gpsimd)
+            multiply_on_scalar(product, j0, pairs_vector, pairs_scalar)
             return product
 
         def quantise_and_contract(product):
@@ -185,6 +192,6 @@ def tile_recon_loss_pa_t_kernel(tc, X, A, B, C_words, C_scales, out):
         step_products = {}
         for step in range(N_STEPS + 1):
             if step < N_STEPS:
-                step_products[step] = multiply(step * J_STEP)
+                step_products[step] = multiply(step)
             if step >= 1:
                 subtract_and_store(step - 1, quantise_and_contract(step_products[step - 1]))

@@ -25,12 +25,14 @@ N_STEPS = N2 // J_STEP
 PAIRS_STEP = J_STEP * PASSES
 
 
+PAIRS_GROUP = J_GROUP * PASSES
+GPSIMD_GROUP = GROUPS - 2
+
+
 def shares(step):
     if step < 2:
-        vector, gpsimd = 19, 4
-    else:
-        vector, gpsimd = 18, 5
-    return vector, PAIRS_STEP - vector - gpsimd, gpsimd
+        return 19, 4
+    return 17, 6
 
 FLOPS = 2 * N1 * N2 * N3 * R
 
@@ -93,7 +95,7 @@ def tile_recon_loss_pa_t_kernel(tc, X, A, B, C_words, C_scales, out):
         bt_f32 = keep.tile([P, N2, PASSES, PACK], F32)
         nc.scalar.copy(out=bt_f32[:], in_=bt[:])
 
-        def multiply_by_tensor_tensor(engine, a_factor, product, j0, first, count):
+        def multiply_in_one_tile(engine, a_factor, product, j0, first, count):
             def one_pair(pair):
                 jl, g = pair // PASSES, pair % PASSES
                 engine.tensor_tensor(
@@ -119,18 +121,30 @@ def tile_recon_loss_pa_t_kernel(tc, X, A, B, C_words, C_scales, out):
             if (last - first) % PASSES:
                 one_pair(last - 1)
 
-        def multiply_on_scalar(product, j0, first, count):
+        def multiply_by_tensor_tensor(engine, a_factor, tiles, j0, first, count):
+            for group in range(GROUPS):
+                low = max(first, group * PAIRS_GROUP)
+                high = min(first + count, (group + 1) * PAIRS_GROUP)
+                if low < high:
+                    multiply_in_one_tile(
+                        engine, a_factor, tiles[group], j0 + group * J_GROUP, low - group * PAIRS_GROUP, high - low
+                    )
+
+        def multiply_on_scalar(tiles, j0, pairs):
+            count = len(pairs)
             planes = products.tile([P, count, PACK, N1], BF16, name="planes")
 
             def group_planes(n):
-                pair = first + n
+                pair = pairs[n] % PAIRS_GROUP
                 nc.scalar.copy(
-                    out=product[:, pair // PASSES, pair % PASSES].rearrange("p (c i) t -> p c t i", i=4),
+                    out=tiles[pairs[n] // PAIRS_GROUP][:, pair // PASSES, pair % PASSES].rearrange(
+                        "p (c i) t -> p c t i", i=4
+                    ),
                     in_=planes[:, n].rearrange("p t (c i) -> p c t i", i=4),
                 )
 
             for n in range(count):
-                pair = first + n
+                pair = pairs[n]
                 for t in range(PACK):
                     nc.scalar.activation(
                         out=planes[:, n, t, :],
@@ -144,14 +158,24 @@ def tile_recon_loss_pa_t_kernel(tc, X, A, B, C_words, C_scales, out):
 
         def multiply(step):
             j0 = step * J_STEP
-            pairs_vector, pairs_scalar, pairs_gpsimd = shares(step)
-            product = products.tile([P, J_STEP, PASSES, N1, PACK], BF16, align_bytes=64, name="product")
-            multiply_by_tensor_tensor(nc.vector, at_in_psum, product, j0, 0, pairs_vector)
-            multiply_by_tensor_tensor(nc.gpsimd, at[:], product, j0, PAIRS_STEP - pairs_gpsimd, pairs_gpsimd)
-            multiply_on_scalar(product, j0, pairs_vector, pairs_scalar)
-            return product
+            pairs_vector, pairs_gpsimd = shares(step)
+            tiles = []
+            for group in range(GROUPS):
+                group_tile = products.tile(
+                    [P, J_GROUP, PASSES, N1, PACK], BF16, align_bytes=64, name="product%d" % group
+                )
+                tiles.append(group_tile)
+            first_gpsimd = (GPSIMD_GROUP + 1) * PAIRS_GROUP - pairs_gpsimd
+            multiply_by_tensor_tensor(nc.vector, at_in_psum, tiles, j0, 0, pairs_vector)
+            multiply_by_tensor_tensor(nc.gpsimd, at[:], tiles, j0, first_gpsimd, pairs_gpsimd)
+            multiply_on_scalar(
+                tiles,
+                j0,
+                list(range(pairs_vector, first_gpsimd)) + list(range(first_gpsimd + pairs_gpsimd, PAIRS_STEP)),
+            )
+            return tiles
 
-        def quantise_and_contract(product):
+        def quantise_and_contract(tiles):
             accs = []
             for group in range(GROUPS):
                 codes = quantised.tile([P, J_GROUP * PASSES * N1], U32, align_bytes=64, name="codes")
@@ -159,9 +183,7 @@ def tile_recon_loss_pa_t_kernel(tc, X, A, B, C_words, C_scales, out):
                 nc.vector.quantize_mx(
                     out=codes[:].bitcast(FP8X4),
                     scales=scales[:],
-                    in_=product[:, group * J_GROUP : (group + 1) * J_GROUP].rearrange(
-                        "p j g i t -> p (j g i t)"
-                    ),
+                    in_=tiles[group][:].rearrange("p j g i t -> p (j g i t)"),
                 )
                 acc = sums.tile([P, J_GROUP, N3], F32, name="acc")
                 for jl in range(J_GROUP):

@@ -31,8 +31,8 @@ GPSIMD_GROUP = GROUPS - 2
 
 def shares(step):
     if step < 2:
-        return 19, 4
-    return 17, 6
+        return 19, 8
+    return 16, 11
 
 FLOPS = 2 * N1 * N2 * N3 * R
 
@@ -130,49 +130,68 @@ def tile_recon_loss_pa_t_kernel(tc, X, A, B, C_words, C_scales, out):
                         engine, a_factor, tiles[group], j0 + group * J_GROUP, low - group * PAIRS_GROUP, high - low
                     )
 
-        def multiply_on_scalar(tiles, j0, pairs):
-            count = len(pairs)
-            planes = products.tile([P, count, PACK, N1], BF16, name="planes")
+        def multiply_half_pair(engine, a_factor, tiles, j0, pair, rows):
+            jl, g = pair // PASSES, pair % PASSES
+            engine.tensor_tensor(
+                out=tiles[pair // PAIRS_GROUP][:, jl % J_GROUP, g, rows],
+                in0=bt[:, j0 + jl, g].unsqueeze(1).to_broadcast([P, rows.stop - rows.start, PACK]),
+                in1=a_factor[:, g, rows],
+                op=mybir.AluOpType.mult,
+            )
 
-            def group_planes(n):
-                pair = pairs[n] % PAIRS_GROUP
+        def multiply_on_scalar(tiles, j0, pieces):
+            count = len(pieces)
+            planes = products.tile([P, count, HALVES, N1, PACK // HALVES], BF16, name="planes")
+
+            def group_words(n):
+                pair, rows = pieces[n]
+                width = rows.stop - rows.start
+                jl, g = pair // PASSES, pair % PASSES
                 nc.scalar.copy(
-                    out=tiles[pairs[n] // PAIRS_GROUP][:, pair // PASSES, pair % PASSES].rearrange(
-                        "p (c i) t -> p c t i", i=4
-                    ),
-                    in_=planes[:, n].rearrange("p t (c i) -> p c t i", i=4),
+                    out=tiles[pair // PAIRS_GROUP][:, jl % J_GROUP, g, rows]
+                    .rearrange("p i t -> p (i t)")
+                    .bitcast(F32)
+                    .rearrange("p (i h) -> p i h", h=HALVES),
+                    in_=planes[:, n, :, 0:width]
+                    .rearrange("p h i e -> p h (i e)")
+                    .bitcast(F32)
+                    .rearrange("p h i -> p i h"),
                 )
 
             for n in range(count):
-                pair = pairs[n]
+                pair, rows = pieces[n]
+                width = rows.stop - rows.start
                 for t in range(PACK):
                     nc.scalar.activation(
-                        out=planes[:, n, t, :],
-                        in_=at[:, pair % PASSES, :, t],
+                        out=planes[:, n, t // HALVES, 0:width, t % HALVES],
+                        in_=at[:, pair % PASSES, rows, t],
                         func=mybir.ActivationFunctionType.Copy,
                         scale=bt_f32[:, j0 + pair // PASSES, pair % PASSES, t : t + 1],
                     )
                 if n > 0:
-                    group_planes(n - 1)
-            group_planes(count - 1)
+                    group_words(n - 1)
+            group_words(count - 1)
 
         def multiply(step):
             j0 = step * J_STEP
-            pairs_vector, pairs_gpsimd = shares(step)
+            pairs_vector, halves_gpsimd = shares(step)
             tiles = []
             for group in range(GROUPS):
                 group_tile = products.tile(
                     [P, J_GROUP, PASSES, N1, PACK], BF16, align_bytes=64, name="product%d" % group
                 )
                 tiles.append(group_tile)
-            first_gpsimd = (GPSIMD_GROUP + 1) * PAIRS_GROUP - pairs_gpsimd
+            end_gpsimd = (GPSIMD_GROUP + 1) * PAIRS_GROUP
+            first_gpsimd = end_gpsimd - halves_gpsimd // 2
+            all_rows, low_rows, high_rows = slice(0, N1), slice(0, N1 // 2), slice(N1 // 2, N1)
+            pieces = [(pair, all_rows) for pair in range(pairs_vector, first_gpsimd - halves_gpsimd % 2)]
             multiply_by_tensor_tensor(nc.vector, at_in_psum, tiles, j0, 0, pairs_vector)
-            multiply_by_tensor_tensor(nc.gpsimd, at[:], tiles, j0, first_gpsimd, pairs_gpsimd)
-            multiply_on_scalar(
-                tiles,
-                j0,
-                list(range(pairs_vector, first_gpsimd)) + list(range(first_gpsimd + pairs_gpsimd, PAIRS_STEP)),
-            )
+            if halves_gpsimd % 2:
+                pieces.append((first_gpsimd - 1, low_rows))
+                multiply_half_pair(nc.gpsimd, at[:], tiles, j0, first_gpsimd - 1, high_rows)
+            multiply_by_tensor_tensor(nc.gpsimd, at[:], tiles, j0, first_gpsimd, end_gpsimd - first_gpsimd)
+            pieces.extend([(pair, all_rows) for pair in range(end_gpsimd, PAIRS_STEP)])
+            multiply_on_scalar(tiles, j0, pieces)
             return tiles
 
         def quantise_and_contract(tiles):

@@ -32,7 +32,9 @@ GPSIMD_GROUP = GROUPS - 2
 def shares(step):
     if step < 2:
         return 19, 8
-    return 16, 11
+    if step == N_STEPS - 1:
+        return 13, 10
+    return 17, 12
 
 FLOPS = 2 * N1 * N2 * N3 * R
 
@@ -194,9 +196,9 @@ def tile_recon_loss_pa_t_kernel(tc, X, A, B, C_words, C_scales, out):
             multiply_on_scalar(tiles, j0, pieces)
             return tiles
 
-        def quantise_and_contract(tiles):
-            accs = []
-            for group in range(GROUPS):
+        def quantise_and_contract(tiles, groups):
+            accs = {}
+            for group in groups:
                 codes = quantised.tile([P, J_GROUP * PASSES * N1], U32, align_bytes=64, name="codes")
                 scales = quantised.tile([P, J_GROUP * PASSES * N1], U8, align_bytes=64, name="scales")
                 nc.vector.quantize_mx(
@@ -217,11 +219,11 @@ def tile_recon_loss_pa_t_kernel(tc, X, A, B, C_words, C_scales, out):
                             start=(g == 0),
                             stop=(g == PASSES - 1),
                         )
-                accs.append(acc)
+                accs[group] = acc
             return accs
 
         def subtract_and_store(step, accs):
-            for group in range(GROUPS):
+            for group in sorted(accs):
                 js = slice(group * J_GROUP, (group + 1) * J_GROUP)
                 result = results.tile([P, J_GROUP, N3], F32, name="result")
                 nc.vector.tensor_tensor(
@@ -231,8 +233,9 @@ def tile_recon_loss_pa_t_kernel(tc, X, A, B, C_words, C_scales, out):
                 nc.sync.dma_start(out=out[:, first : first + J_GROUP, :], in_=result[:])
 
         step_products = {}
-        for step in range(N_STEPS + 1):
-            if step < N_STEPS:
-                step_products[step] = multiply(step)
+        for step in range(N_STEPS):
+            step_products[step] = multiply(step)
             if step >= 1:
-                subtract_and_store(step - 1, quantise_and_contract(step_products[step - 1]))
+                subtract_and_store(step - 1, quantise_and_contract(step_products[step - 1], range(GROUPS)))
+        subtract_and_store(N_STEPS - 1, quantise_and_contract(step_products[N_STEPS - 1], range(GROUPS - 1)))
+        subtract_and_store(N_STEPS - 1, quantise_and_contract(step_products[N_STEPS - 1], [GROUPS - 1]))

@@ -196,16 +196,18 @@ def tile_recon_loss_pa_t_kernel(tc, X, A, B, C_words, C_scales, out):
             multiply_on_scalar(tiles, j0, pieces)
             return tiles
 
-        def quantise_and_contract(tiles, groups):
+        def quantise_and_contract(tiles, groups, cuts=1):
             accs = {}
             for group in groups:
                 codes = quantised.tile([P, J_GROUP * PASSES * N1], U32, align_bytes=64, name="codes")
                 scales = quantised.tile([P, J_GROUP * PASSES * N1], U8, align_bytes=64, name="scales")
-                nc.vector.quantize_mx(
-                    out=codes[:].bitcast(FP8X4),
-                    scales=scales[:],
-                    in_=tiles[group][:].rearrange("p j g i t -> p (j g i t)"),
-                )
+                js, words = J_GROUP // cuts, J_GROUP * PASSES * N1 // cuts
+                for cut in range(cuts):
+                    nc.vector.quantize_mx(
+                        out=codes[:, cut * words : (cut + 1) * words].bitcast(FP8X4),
+                        scales=scales[:, cut * words : (cut + 1) * words],
+                        in_=tiles[group][:, cut * js : (cut + 1) * js].rearrange("p j g i t -> p (j g i t)"),
+                    )
                 acc = sums.tile([P, J_GROUP, N3], F32, name="acc")
                 for jl in range(J_GROUP):
                     for g in range(PASSES):
@@ -237,5 +239,9 @@ def tile_recon_loss_pa_t_kernel(tc, X, A, B, C_words, C_scales, out):
             step_products[step] = multiply(step)
             if step >= 1:
                 subtract_and_store(step - 1, quantise_and_contract(step_products[step - 1], range(GROUPS)))
-        subtract_and_store(N_STEPS - 1, quantise_and_contract(step_products[N_STEPS - 1], range(GROUPS - 1)))
-        subtract_and_store(N_STEPS - 1, quantise_and_contract(step_products[N_STEPS - 1], [GROUPS - 1]))
+        last = step_products[N_STEPS - 1]
+        early = quantise_and_contract(last, range(GROUPS - 1))
+        subtract_and_store(N_STEPS - 1, {group: early[group] for group in range(GROUPS - 2)})
+        late = quantise_and_contract(last, [GROUPS - 1], cuts=2)
+        late[GROUPS - 2] = early[GROUPS - 2]
+        subtract_and_store(N_STEPS - 1, late)

@@ -49,15 +49,21 @@ def tile_recon_loss_pa_t_kernel(tc, X, A, B, C_words, C_scales, out):
         quantised = stack.enter_context(tc.tile_pool(name="quantised", bufs=GROUPS + 1))
         results = stack.enter_context(tc.tile_pool(name="results", bufs=GROUPS + 2))
         turned = stack.enter_context(tc.psum_pool(name="turned", bufs=1))
-        sums = stack.enter_context(tc.psum_pool(name="sums", bufs=GROUPS))
+        sums = stack.enter_context(tc.psum_pool(name="sums", bufs=7))
 
         w_scales = keep.tile([P, PASSES, N3], U8, align_bytes=64)
         nc.vector.memset(w_scales[:].bitcast(I32), 0)
 
-        a_rows = keep.tile([N1, R], BF16)
-        b_rows = keep.tile([N2, R], BF16)
-        nc.sync.dma_start(out=b_rows[:], in_=B)
-        nc.scalar.dma_start(out=a_rows[:], in_=A)
+        a_rows, b_rows = [], []
+        for g in range(PASSES):
+            half = slice(g * (R // PASSES), (g + 1) * (R // PASSES))
+            queue = (nc.sync, nc.scalar)[g]
+            b_piece = keep.tile([N2, R // PASSES], BF16, name="b_rows%d" % g)
+            queue.dma_start(out=b_piece[:], in_=B[:, half])
+            b_rows.append(b_piece)
+            a_piece = keep.tile([N1, R // PASSES], BF16, name="a_rows%d" % g)
+            queue.dma_start(out=a_piece[:], in_=A[:, half])
+            a_rows.append(a_piece)
 
         w_words = keep.tile([P, PASSES, 2 * N3], U8, align_bytes=64)
         nc.sync.dma_start(
@@ -79,23 +85,38 @@ def tile_recon_loss_pa_t_kernel(tc, X, A, B, C_words, C_scales, out):
 
         identity = keep.tile([P, P], F32)
         make_identity(nc, identity[:])
-        b_turned = turned.tile([P, N2, PASSES, HALVES], F32)
-        a_turned = turned.tile([P, PASSES, N1, HALVES], F32)
-        for g in range(PASSES):
+
+        def turn(rows, columns_out):
             for h in range(HALVES):
-                columns = slice(g * (WORDS // PASSES) + h, (g + 1) * (WORDS // PASSES), HALVES)
-                nc.tensor.transpose(b_turned[:, :, g, h], b_rows[:].bitcast(F32)[:, columns], identity[:])
-        for g in range(PASSES):
-            for h in range(HALVES):
-                columns = slice(g * (WORDS // PASSES) + h, (g + 1) * (WORDS // PASSES), HALVES)
-                nc.tensor.transpose(a_turned[:, g, :, h], a_rows[:].bitcast(F32)[:, columns], identity[:])
+                nc.tensor.transpose(columns_out[:, :, h], rows[:].bitcast(F32)[:, h::HALVES], identity[:])
+
         bt = keep.tile([P, N2, PASSES, PACK], BF16)
         at = keep.tile([P, PASSES, N1, PACK], BF16)
-        nc.vector.tensor_copy(out=bt[:].bitcast(F32), in_=b_turned[:])
-        nc.vector.tensor_copy(out=at[:].bitcast(F32), in_=a_turned[:])
+
+        bank = [P, J_GROUP * N3]
+        b_bank = sums.tile(bank, F32, name="acc")
+        b_turned = b_bank[:].rearrange("p (n g h) -> p n g h", g=PASSES, h=HALVES)
+        for g in range(PASSES):
+            turn(b_rows[g], b_turned[:, :, g])
+        nc.vector.tensor_copy(out=bt[:].rearrange("p n g t -> p (n g t)").bitcast(F32), in_=b_bank[:])
+        a_first = []
+        for g in range(PASSES):
+            a_bank = sums.tile(bank, F32, name="acc")
+            a_words = a_bank[:, 0 : N1 * HALVES]
+            turn(a_rows[g], a_words.rearrange("p (n h) -> p n h", h=HALVES))
+            nc.scalar.copy(out=at[:, g].rearrange("p n t -> p (n t)").bitcast(F32), in_=a_words)
+            a_first.append(a_words.bitcast(BF16).rearrange("p (n t) -> p n t", t=PACK))
+        a_turned = turned.tile([P, PASSES, N1, HALVES], F32)
+        for g in range(PASSES):
+            turn(a_rows[g], a_turned[:, g])
         at_in_psum = a_turned[:].bitcast(BF16)
         bt_f32 = keep.tile([P, N2, PASSES, PACK], F32)
-        nc.scalar.copy(out=bt_f32[:], in_=bt[:])
+
+        def convert_for_scalar(steps, j_range):
+            nc.scalar.copy(
+                out=bt_f32[:].rearrange("p (s j) g t -> p s j g t", j=J_STEP)[:, steps, j_range],
+                in_=bt[:].rearrange("p (s j) g t -> p s j g t", j=J_STEP)[:, steps, j_range],
+            )
 
         def multiply_in_one_tile(engine, a_factor, product, j0, first, count):
             def one_pair(pair):
@@ -131,6 +152,21 @@ def tile_recon_loss_pa_t_kernel(tc, X, A, B, C_words, C_scales, out):
                     multiply_in_one_tile(
                         engine, a_factor, tiles[group], j0 + group * J_GROUP, low - group * PAIRS_GROUP, high - low
                     )
+
+        def multiply_pass_by_pass(tiles, count):
+            for g in range(PASSES):
+                values = (count - g + 1) // PASSES
+                for group in range(GROUPS):
+                    width = min(values - group * J_GROUP, J_GROUP)
+                    if width > 0:
+                        shape = [P, width, N1, PACK]
+                        js = slice(group * J_GROUP, group * J_GROUP + width)
+                        nc.vector.tensor_tensor(
+                            out=tiles[group][:, 0:width, g],
+                            in0=bt[:, js, g].unsqueeze(2).to_broadcast(shape),
+                            in1=a_first[g].unsqueeze(1).to_broadcast(shape),
+                            op=mybir.AluOpType.mult,
+                        )
 
         def multiply_half_pair(engine, a_factor, tiles, j0, pair, rows):
             jl, g = pair // PASSES, pair % PASSES
@@ -187,13 +223,20 @@ def tile_recon_loss_pa_t_kernel(tc, X, A, B, C_words, C_scales, out):
             first_gpsimd = end_gpsimd - halves_gpsimd // 2
             all_rows, low_rows, high_rows = slice(0, N1), slice(0, N1 // 2), slice(N1 // 2, N1)
             pieces = [(pair, all_rows) for pair in range(pairs_vector, first_gpsimd - halves_gpsimd % 2)]
-            multiply_by_tensor_tensor(nc.vector, at_in_psum, tiles, j0, 0, pairs_vector)
+            if step == 0:
+                multiply_pass_by_pass(tiles, pairs_vector)
+            else:
+                multiply_by_tensor_tensor(nc.vector, at_in_psum, tiles, j0, 0, pairs_vector)
             if halves_gpsimd % 2:
                 pieces.append((first_gpsimd - 1, low_rows))
                 multiply_half_pair(nc.gpsimd, at[:], tiles, j0, first_gpsimd - 1, high_rows)
             multiply_by_tensor_tensor(nc.gpsimd, at[:], tiles, j0, first_gpsimd, end_gpsimd - first_gpsimd)
             pieces.extend([(pair, all_rows) for pair in range(end_gpsimd, PAIRS_STEP)])
+            if step == 0:
+                convert_for_scalar(slice(0, 1), slice(pieces[0][0] // PASSES, J_STEP))
             multiply_on_scalar(tiles, j0, pieces)
+            if step == 0:
+                convert_for_scalar(slice(1, N_STEPS), slice(min(shares(n)[0] for n in range(1, N_STEPS)) // PASSES, J_STEP))
             return tiles
 
         def quantise_and_contract(tiles, groups, cuts=1):

@@ -31,10 +31,17 @@ GPSIMD_GROUP = GROUPS - 2
 
 def shares(step):
     if step < 2:
-        return 19, 8
+        return 20, 0, 8
     if step == N_STEPS - 1:
-        return 13, 10
-    return 17, 12
+        return 20, 0, 6
+    return 23, step % 2, 2
+
+
+def subtracts_on_gpsimd(step):
+    return step < N_STEPS - 2
+
+
+SCALAR_FIRST = 4
 
 FLOPS = 2 * N1 * N2 * N3 * R
 
@@ -90,6 +97,15 @@ def tile_recon_loss_pa_t_kernel(tc, X, A, B, C_words, C_scales, out):
             for h in range(HALVES):
                 nc.tensor.transpose(columns_out[:, :, h], rows[:].bitcast(F32)[:, h::HALVES], identity[:])
 
+        def product_tiles():
+            tiles = []
+            for group in range(GROUPS):
+                group_tile = products.tile(
+                    [P, J_GROUP, PASSES, N1, PACK], BF16, align_bytes=64, name="product%d" % group
+                )
+                tiles.append(group_tile)
+            return tiles
+
         bt = keep.tile([P, N2, PASSES, PACK], BF16)
         at = keep.tile([P, PASSES, N1, PACK], BF16)
 
@@ -98,14 +114,27 @@ def tile_recon_loss_pa_t_kernel(tc, X, A, B, C_words, C_scales, out):
         b_turned = b_bank[:].rearrange("p (n g h) -> p n g h", g=PASSES, h=HALVES)
         for g in range(PASSES):
             turn(b_rows[g], b_turned[:, :, g])
-        nc.vector.tensor_copy(out=bt[:].rearrange("p n g t -> p (n g t)").bitcast(F32), in_=b_bank[:])
-        a_first = []
+        bt_words = bt[:].rearrange("p n g t -> p (n g t)").bitcast(F32)
+        cut = J_STEP * PASSES * HALVES
+        nc.vector.tensor_copy(out=bt_words[:, 0:cut], in_=b_bank[:, 0:cut])
+        nc.vector.tensor_copy(out=bt_words[:, cut:], in_=b_bank[:, cut:])
+        step_0 = product_tiles()
         for g in range(PASSES):
             a_bank = sums.tile(bank, F32, name="acc")
             a_words = a_bank[:, 0 : N1 * HALVES]
             turn(a_rows[g], a_words.rearrange("p (n h) -> p n h", h=HALVES))
             nc.scalar.copy(out=at[:, g].rearrange("p n t -> p (n t)").bitcast(F32), in_=a_words)
-            a_first.append(a_words.bitcast(BF16).rearrange("p (n t) -> p n t", t=PACK))
+            a_factor = a_words.bitcast(BF16).rearrange("p (n t) -> p n t", t=PACK)
+            values = (shares(0)[0] - g + 1) // PASSES
+            for first in range(0, values, J_GROUP):
+                width = min(J_GROUP, values - first)
+                shape = [P, width, N1, PACK]
+                nc.vector.tensor_tensor(
+                    out=step_0[first // J_GROUP][:, 0:width, g],
+                    in0=bt[:, first : first + width, g].unsqueeze(2).to_broadcast(shape),
+                    in1=a_factor.unsqueeze(1).to_broadcast(shape),
+                    op=mybir.AluOpType.mult,
+                )
         a_turned = turned.tile([P, PASSES, N1, HALVES], F32)
         for g in range(PASSES):
             turn(a_rows[g], a_turned[:, g])
@@ -153,21 +182,6 @@ def tile_recon_loss_pa_t_kernel(tc, X, A, B, C_words, C_scales, out):
                         engine, a_factor, tiles[group], j0 + group * J_GROUP, low - group * PAIRS_GROUP, high - low
                     )
 
-        def multiply_pass_by_pass(tiles, count):
-            for g in range(PASSES):
-                values = (count - g + 1) // PASSES
-                for group in range(GROUPS):
-                    width = min(values - group * J_GROUP, J_GROUP)
-                    if width > 0:
-                        shape = [P, width, N1, PACK]
-                        js = slice(group * J_GROUP, group * J_GROUP + width)
-                        nc.vector.tensor_tensor(
-                            out=tiles[group][:, 0:width, g],
-                            in0=bt[:, js, g].unsqueeze(2).to_broadcast(shape),
-                            in1=a_first[g].unsqueeze(1).to_broadcast(shape),
-                            op=mybir.AluOpType.mult,
-                        )
-
         def multiply_half_pair(engine, a_factor, tiles, j0, pair, rows):
             jl, g = pair // PASSES, pair % PASSES
             engine.tensor_tensor(
@@ -196,48 +210,44 @@ def tile_recon_loss_pa_t_kernel(tc, X, A, B, C_words, C_scales, out):
                     .rearrange("p h i -> p i h"),
                 )
 
-            for n in range(count):
-                pair, rows = pieces[n]
-                width = rows.stop - rows.start
-                for t in range(PACK):
-                    nc.scalar.activation(
-                        out=planes[:, n, t // HALVES, 0:width, t % HALVES],
-                        in_=at[:, pair % PASSES, rows, t],
-                        func=mybir.ActivationFunctionType.Copy,
-                        scale=bt_f32[:, j0 + pair // PASSES, pair % PASSES, t : t + 1],
-                    )
-                if n > 0:
-                    group_words(n - 1)
-            group_words(count - 1)
+            def run(low, high):
+                for n in range(low, high):
+                    pair, rows = pieces[n]
+                    width = rows.stop - rows.start
+                    for t in range(PACK):
+                        nc.scalar.activation(
+                            out=planes[:, n, t // HALVES, 0:width, t % HALVES],
+                            in_=at[:, pair % PASSES, rows, t],
+                            func=mybir.ActivationFunctionType.Copy,
+                            scale=bt_f32[:, j0 + pair // PASSES, pair % PASSES, t : t + 1],
+                        )
+                    if n > 0:
+                        group_words(n - 1)
+                if high == count:
+                    group_words(count - 1)
+
+            return run, count
 
         def multiply(step):
             j0 = step * J_STEP
-            pairs_vector, halves_gpsimd = shares(step)
-            tiles = []
-            for group in range(GROUPS):
-                group_tile = products.tile(
-                    [P, J_GROUP, PASSES, N1, PACK], BF16, align_bytes=64, name="product%d" % group
-                )
-                tiles.append(group_tile)
+            pairs_vector, extra_vector, halves_gpsimd = shares(step)
+            tiles = product_tiles() if step else step_0
             end_gpsimd = (GPSIMD_GROUP + 1) * PAIRS_GROUP
             first_gpsimd = end_gpsimd - halves_gpsimd // 2
             all_rows, low_rows, high_rows = slice(0, N1), slice(0, N1 // 2), slice(N1 // 2, N1)
             pieces = [(pair, all_rows) for pair in range(pairs_vector, first_gpsimd - halves_gpsimd % 2)]
-            if step == 0:
-                multiply_pass_by_pass(tiles, pairs_vector)
-            else:
+            if step:
                 multiply_by_tensor_tensor(nc.vector, at_in_psum, tiles, j0, 0, pairs_vector)
+            multiply_by_tensor_tensor(nc.vector, at_in_psum, tiles, j0, end_gpsimd, extra_vector)
             if halves_gpsimd % 2:
                 pieces.append((first_gpsimd - 1, low_rows))
                 multiply_half_pair(nc.gpsimd, at[:], tiles, j0, first_gpsimd - 1, high_rows)
             multiply_by_tensor_tensor(nc.gpsimd, at[:], tiles, j0, first_gpsimd, end_gpsimd - first_gpsimd)
-            pieces.extend([(pair, all_rows) for pair in range(end_gpsimd, PAIRS_STEP)])
+            pieces.extend([(pair, all_rows) for pair in range(end_gpsimd + extra_vector, PAIRS_STEP)])
             if step == 0:
                 convert_for_scalar(slice(0, 1), slice(pieces[0][0] // PASSES, J_STEP))
-            multiply_on_scalar(tiles, j0, pieces)
-            if step == 0:
-                convert_for_scalar(slice(1, N_STEPS), slice(min(shares(n)[0] for n in range(1, N_STEPS)) // PASSES, J_STEP))
-            return tiles
+            scalar_run, count = multiply_on_scalar(tiles, j0, pieces)
+            return tiles, scalar_run, count
 
         def quantise_and_contract(tiles, groups, cuts=1):
             accs = {}
@@ -267,24 +277,58 @@ def tile_recon_loss_pa_t_kernel(tc, X, A, B, C_words, C_scales, out):
                 accs[group] = acc
             return accs
 
-        def subtract_and_store(step, accs):
+        def subtract_and_store(step, accs, cuts=1):
+            width = J_GROUP // cuts
             for group in sorted(accs):
-                js = slice(group * J_GROUP, (group + 1) * J_GROUP)
-                result = results.tile([P, J_GROUP, N3], F32, name="result")
-                nc.vector.tensor_tensor(
-                    out=result[:], in0=accs[group][:], in1=x_steps[step][:, js, :], op=mybir.AluOpType.subtract
-                )
-                first = step * J_STEP + group * J_GROUP
-                nc.sync.dma_start(out=out[:, first : first + J_GROUP, :], in_=result[:])
+                for cut in range(cuts):
+                    own = slice(cut * width, (cut + 1) * width)
+                    js = slice(group * J_GROUP + own.start, group * J_GROUP + own.stop)
+                    result = results.tile([P, width, N3], F32, name="result")
+                    nc.vector.tensor_tensor(
+                        out=result[:], in0=accs[group][:, own], in1=x_steps[step][:, js, :], op=mybir.AluOpType.subtract
+                    )
+                    nc.sync.dma_start(
+                        out=out[:, step * J_STEP + js.start : step * J_STEP + js.stop, :], in_=result[:]
+                    )
 
-        step_products = {}
+        def copy_sums(accs):
+            copies = {}
+            for group in sorted(accs):
+                copied = results.tile([P, J_GROUP, N3], F32, name="copied", bufs=2 * GROUPS)
+                nc.scalar.copy(out=copied[:], in_=accs[group][:])
+                copies[group] = copied
+            return copies
+
+        def subtract_copied_and_store(step, copies):
+            for group in sorted(copies):
+                js = slice(group * J_GROUP, (group + 1) * J_GROUP)
+                copied = copies[group]
+                nc.gpsimd.tensor_tensor(
+                    out=copied[:], in0=copied[:], in1=x_steps[step][:, js, :], op=mybir.AluOpType.subtract
+                )
+                first = step * J_STEP + js.start
+                nc.sync.dma_start(out=out[:, first : first + J_GROUP, :], in_=copied[:])
+
+        step_products, copied_sums = {}, {}
         for step in range(N_STEPS):
-            step_products[step] = multiply(step)
-            if step >= 1:
-                subtract_and_store(step - 1, quantise_and_contract(step_products[step - 1], range(GROUPS)))
+            step_products[step], scalar_run, count = multiply(step)
+            if step - 2 in copied_sums:
+                subtract_copied_and_store(step - 2, copied_sums[step - 2])
+            if step == 0:
+                scalar_run(0, count)
+                fronts = [shares(n)[0] for n in range(1, N_STEPS)]
+                convert_for_scalar(slice(1, N_STEPS), slice(min(fronts) // PASSES, J_STEP))
+                continue
+            scalar_run(0, SCALAR_FIRST)
+            accs = quantise_and_contract(step_products[step - 1], range(GROUPS))
+            if subtracts_on_gpsimd(step - 1):
+                copied_sums[step - 1] = copy_sums(accs)
+            else:
+                subtract_and_store(step - 1, accs)
+            scalar_run(SCALAR_FIRST, count)
         last = step_products[N_STEPS - 1]
         early = quantise_and_contract(last, range(GROUPS - 1))
         subtract_and_store(N_STEPS - 1, {group: early[group] for group in range(GROUPS - 2)})
         late = quantise_and_contract(last, [GROUPS - 1], cuts=2)
-        late[GROUPS - 2] = early[GROUPS - 2]
-        subtract_and_store(N_STEPS - 1, late)
+        subtract_and_store(N_STEPS - 1, {GROUPS - 2: early[GROUPS - 2]})
+        subtract_and_store(N_STEPS - 1, late, cuts=2)

@@ -41,6 +41,7 @@ def subtracts_on_gpsimd(step):
     return step < N_STEPS - 2
 
 
+COPIES = 2
 SCALAR_FIRST = 4
 
 FLOPS = 2 * N1 * N2 * N3 * R
@@ -292,22 +293,24 @@ def tile_recon_loss_pa_t_kernel(tc, X, A, B, C_words, C_scales, out):
                     )
 
         def copy_sums(accs):
-            copies = {}
+            copies = []
             for group in sorted(accs):
-                copied = results.tile([P, J_GROUP, N3], F32, name="copied", bufs=2 * GROUPS)
-                nc.scalar.copy(out=copied[:], in_=accs[group][:])
-                copies[group] = copied
+                if group % COPIES == 0:
+                    copied = results.tile([P, COPIES * J_GROUP, N3], F32, name="copied", bufs=2 * GROUPS // COPIES)
+                    copies.append(copied)
+                first = (group % COPIES) * J_GROUP
+                nc.scalar.copy(out=copied[:, first : first + J_GROUP, :], in_=accs[group][:])
             return copies
 
         def subtract_copied_and_store(step, copies):
-            for group in sorted(copies):
-                js = slice(group * J_GROUP, (group + 1) * J_GROUP)
-                copied = copies[group]
+            width = COPIES * J_GROUP
+            for n, copied in enumerate(copies):
+                js = slice(n * width, (n + 1) * width)
                 nc.gpsimd.tensor_tensor(
                     out=copied[:], in0=copied[:], in1=x_steps[step][:, js, :], op=mybir.AluOpType.subtract
                 )
                 first = step * J_STEP + js.start
-                nc.sync.dma_start(out=out[:, first : first + J_GROUP, :], in_=copied[:])
+                nc.sync.dma_start(out=out[:, first : first + width, :], in_=copied[:])
 
         step_products, copied_sums = {}, {}
         for step in range(N_STEPS):

@@ -23,18 +23,16 @@ J_STEP = 16
 GROUPS = J_STEP // J_GROUP
 N_STEPS = N2 // J_STEP
 PAIRS_STEP = J_STEP * PASSES
-
-
 PAIRS_GROUP = J_GROUP * PASSES
 GPSIMD_GROUP = GROUPS - 2
 
 
 def shares(step):
     if step < 2:
-        return 20, 0, 8
+        return 20, 0, 4
     if step == N_STEPS - 1:
-        return 20, 0, 6
-    return 23, step % 2, 2
+        return 20, 0, 2
+    return 23, (step + 1) % 2, 1
 
 
 def subtracts_on_gpsimd(step):
@@ -65,12 +63,11 @@ def tile_recon_loss_pa_t_kernel(tc, X, A, B, C_words, C_scales, out):
         a_rows, b_rows = [], []
         for g in range(PASSES):
             half = slice(g * (R // PASSES), (g + 1) * (R // PASSES))
-            queue = (nc.sync, nc.scalar)[g]
             b_piece = keep.tile([N2, R // PASSES], BF16, name="b_rows%d" % g)
-            queue.dma_start(out=b_piece[:], in_=B[:, half])
+            nc.sync.dma_start(out=b_piece[:], in_=B[:, half])
             b_rows.append(b_piece)
             a_piece = keep.tile([N1, R // PASSES], BF16, name="a_rows%d" % g)
-            queue.dma_start(out=a_piece[:], in_=A[:, half])
+            nc.scalar.dma_start(out=a_piece[:], in_=A[:, half])
             a_rows.append(a_piece)
 
         w_words = keep.tile([P, PASSES, 2 * N3], U8, align_bytes=64)
@@ -93,10 +90,31 @@ def tile_recon_loss_pa_t_kernel(tc, X, A, B, C_words, C_scales, out):
 
         identity = keep.tile([P, P], F32)
         make_identity(nc, identity[:])
+        bt = keep.tile([P, N2, PASSES, PACK], BF16)
+        at = keep.tile([P, PASSES, N1, PACK], BF16)
+        bt_f32 = keep.tile([P, N2, PASSES, PACK], F32)
+        a_turned = turned.tile([P, PASSES, N1, HALVES], F32)
+        at_in_psum = a_turned[:].bitcast(BF16)
 
-        def turn(rows, columns_out):
+        def turn(rows, words_out):
             for h in range(HALVES):
-                nc.tensor.transpose(columns_out[:, :, h], rows[:].bitcast(F32)[:, h::HALVES], identity[:])
+                nc.tensor.transpose(words_out[:, :, h], rows[:].bitcast(F32)[:, h::HALVES], identity[:])
+
+        def turned_bank(rows):
+            bank = sums.tile([P, J_GROUP * N3], F32, name="acc")
+            words = bank[:, 0 : N1 * HALVES]
+            turn(rows, words.rearrange("p (n h) -> p n h", h=HALVES))
+            return words
+
+        def as_words(factor):
+            return factor.bitcast(F32)
+
+        def convert_for_scalar(steps, first_pair, passes):
+            js = slice(first_pair // PASSES, J_STEP)
+            nc.scalar.copy(
+                out=bt_f32[:].rearrange("p (s j) g t -> p s j g t", j=J_STEP)[:, steps, js, passes],
+                in_=bt[:].rearrange("p (s j) g t -> p s j g t", j=J_STEP)[:, steps, js, passes],
+            )
 
         def product_tiles():
             tiles = []
@@ -107,48 +125,7 @@ def tile_recon_loss_pa_t_kernel(tc, X, A, B, C_words, C_scales, out):
                 tiles.append(group_tile)
             return tiles
 
-        bt = keep.tile([P, N2, PASSES, PACK], BF16)
-        at = keep.tile([P, PASSES, N1, PACK], BF16)
-
-        bank = [P, J_GROUP * N3]
-        b_bank = sums.tile(bank, F32, name="acc")
-        b_turned = b_bank[:].rearrange("p (n g h) -> p n g h", g=PASSES, h=HALVES)
-        for g in range(PASSES):
-            turn(b_rows[g], b_turned[:, :, g])
-        bt_words = bt[:].rearrange("p n g t -> p (n g t)").bitcast(F32)
-        cut = J_STEP * PASSES * HALVES
-        nc.vector.tensor_copy(out=bt_words[:, 0:cut], in_=b_bank[:, 0:cut])
-        nc.vector.tensor_copy(out=bt_words[:, cut:], in_=b_bank[:, cut:])
-        step_0 = product_tiles()
-        for g in range(PASSES):
-            a_bank = sums.tile(bank, F32, name="acc")
-            a_words = a_bank[:, 0 : N1 * HALVES]
-            turn(a_rows[g], a_words.rearrange("p (n h) -> p n h", h=HALVES))
-            nc.scalar.copy(out=at[:, g].rearrange("p n t -> p (n t)").bitcast(F32), in_=a_words)
-            a_factor = a_words.bitcast(BF16).rearrange("p (n t) -> p n t", t=PACK)
-            values = (shares(0)[0] - g + 1) // PASSES
-            for first in range(0, values, J_GROUP):
-                width = min(J_GROUP, values - first)
-                shape = [P, width, N1, PACK]
-                nc.vector.tensor_tensor(
-                    out=step_0[first // J_GROUP][:, 0:width, g],
-                    in0=bt[:, first : first + width, g].unsqueeze(2).to_broadcast(shape),
-                    in1=a_factor.unsqueeze(1).to_broadcast(shape),
-                    op=mybir.AluOpType.mult,
-                )
-        a_turned = turned.tile([P, PASSES, N1, HALVES], F32)
-        for g in range(PASSES):
-            turn(a_rows[g], a_turned[:, g])
-        at_in_psum = a_turned[:].bitcast(BF16)
-        bt_f32 = keep.tile([P, N2, PASSES, PACK], F32)
-
-        def convert_for_scalar(steps, j_range):
-            nc.scalar.copy(
-                out=bt_f32[:].rearrange("p (s j) g t -> p s j g t", j=J_STEP)[:, steps, j_range],
-                in_=bt[:].rearrange("p (s j) g t -> p s j g t", j=J_STEP)[:, steps, j_range],
-            )
-
-        def multiply_in_one_tile(engine, a_factor, product, j0, first, count):
+        def multiply_in_one_tile(engine, a_factor, product, j0, first, last):
             def one_pair(pair):
                 jl, g = pair // PASSES, pair % PASSES
                 engine.tensor_tensor(
@@ -158,7 +135,6 @@ def tile_recon_loss_pa_t_kernel(tc, X, A, B, C_words, C_scales, out):
                     op=mybir.AluOpType.mult,
                 )
 
-            last = first + count
             if first % PASSES:
                 one_pair(first)
                 first += 1
@@ -174,38 +150,36 @@ def tile_recon_loss_pa_t_kernel(tc, X, A, B, C_words, C_scales, out):
             if (last - first) % PASSES:
                 one_pair(last - 1)
 
-        def multiply_by_tensor_tensor(engine, a_factor, tiles, j0, first, count):
+        def multiply(engine, a_factor, tiles, j0, first, last):
             for group in range(GROUPS):
-                low = max(first, group * PAIRS_GROUP)
-                high = min(first + count, (group + 1) * PAIRS_GROUP)
+                start = group * PAIRS_GROUP
+                low, high = max(first - start, 0), min(last - start, PAIRS_GROUP)
                 if low < high:
-                    multiply_in_one_tile(
-                        engine, a_factor, tiles[group], j0 + group * J_GROUP, low - group * PAIRS_GROUP, high - low
-                    )
+                    multiply_in_one_tile(engine, a_factor, tiles[group], j0 + group * J_GROUP, low, high)
 
-        def multiply_half_pair(engine, a_factor, tiles, j0, pair, rows):
-            jl, g = pair // PASSES, pair % PASSES
-            engine.tensor_tensor(
-                out=tiles[pair // PAIRS_GROUP][:, jl % J_GROUP, g, rows],
-                in0=bt[:, j0 + jl, g].unsqueeze(1).to_broadcast([P, rows.stop - rows.start, PACK]),
-                in1=a_factor[:, g, rows],
-                op=mybir.AluOpType.mult,
-            )
+        END_GPSIMD = (GPSIMD_GROUP + 1) * PAIRS_GROUP
 
-        def multiply_on_scalar(tiles, j0, pieces):
-            count = len(pieces)
-            planes = products.tile([P, count, HALVES, N1, PACK // HALVES], BF16, name="planes")
+        def multiply_on_vector(step, tiles):
+            front, extra, unused = shares(step)
+            multiply(nc.vector, at_in_psum, tiles, step * J_STEP, 0, front)
+            multiply(nc.vector, at_in_psum, tiles, step * J_STEP, END_GPSIMD, END_GPSIMD + extra)
+
+        def multiply_on_gpsimd(step, tiles):
+            multiply(nc.gpsimd, at[:], tiles, step * J_STEP, END_GPSIMD - shares(step)[2], END_GPSIMD)
+
+        def scalar_pairs(step):
+            front, extra, gpsimd = shares(step)
+            return list(range(front, END_GPSIMD - gpsimd)) + list(range(END_GPSIMD + extra, PAIRS_STEP))
+
+        def multiply_on_scalar(step, tiles, pairs):
+            planes = products.tile([P, len(pairs), HALVES, N1, PACK // HALVES], BF16, name="planes")
 
             def group_words(n):
-                pair, rows = pieces[n]
-                width = rows.stop - rows.start
-                jl, g = pair // PASSES, pair % PASSES
+                pair = pairs[n]
+                product = tiles[pair // PAIRS_GROUP][:, (pair // PASSES) % J_GROUP, pair % PASSES]
                 nc.scalar.copy(
-                    out=tiles[pair // PAIRS_GROUP][:, jl % J_GROUP, g, rows]
-                    .rearrange("p i t -> p (i t)")
-                    .bitcast(F32)
-                    .rearrange("p (i h) -> p i h", h=HALVES),
-                    in_=planes[:, n, :, 0:width]
+                    out=product.rearrange("p i t -> p (i t)").bitcast(F32).rearrange("p (i h) -> p i h", h=HALVES),
+                    in_=planes[:, n]
                     .rearrange("p h i e -> p h (i e)")
                     .bitcast(F32)
                     .rearrange("p h i -> p i h"),
@@ -213,42 +187,20 @@ def tile_recon_loss_pa_t_kernel(tc, X, A, B, C_words, C_scales, out):
 
             def run(low, high):
                 for n in range(low, high):
-                    pair, rows = pieces[n]
-                    width = rows.stop - rows.start
+                    j, g = step * J_STEP + pairs[n] // PASSES, pairs[n] % PASSES
                     for t in range(PACK):
                         nc.scalar.activation(
-                            out=planes[:, n, t // HALVES, 0:width, t % HALVES],
-                            in_=at[:, pair % PASSES, rows, t],
+                            out=planes[:, n, t // HALVES, :, t % HALVES],
+                            in_=at[:, g, :, t],
                             func=mybir.ActivationFunctionType.Copy,
-                            scale=bt_f32[:, j0 + pair // PASSES, pair % PASSES, t : t + 1],
+                            scale=bt_f32[:, j, g, t : t + 1],
                         )
                     if n > 0:
                         group_words(n - 1)
-                if high == count:
-                    group_words(count - 1)
+                if high == len(pairs):
+                    group_words(high - 1)
 
-            return run, count
-
-        def multiply(step):
-            j0 = step * J_STEP
-            pairs_vector, extra_vector, halves_gpsimd = shares(step)
-            tiles = product_tiles() if step else step_0
-            end_gpsimd = (GPSIMD_GROUP + 1) * PAIRS_GROUP
-            first_gpsimd = end_gpsimd - halves_gpsimd // 2
-            all_rows, low_rows, high_rows = slice(0, N1), slice(0, N1 // 2), slice(N1 // 2, N1)
-            pieces = [(pair, all_rows) for pair in range(pairs_vector, first_gpsimd - halves_gpsimd % 2)]
-            if step:
-                multiply_by_tensor_tensor(nc.vector, at_in_psum, tiles, j0, 0, pairs_vector)
-            multiply_by_tensor_tensor(nc.vector, at_in_psum, tiles, j0, end_gpsimd, extra_vector)
-            if halves_gpsimd % 2:
-                pieces.append((first_gpsimd - 1, low_rows))
-                multiply_half_pair(nc.gpsimd, at[:], tiles, j0, first_gpsimd - 1, high_rows)
-            multiply_by_tensor_tensor(nc.gpsimd, at[:], tiles, j0, first_gpsimd, end_gpsimd - first_gpsimd)
-            pieces.extend([(pair, all_rows) for pair in range(end_gpsimd + extra_vector, PAIRS_STEP)])
-            if step == 0:
-                convert_for_scalar(slice(0, 1), slice(pieces[0][0] // PASSES, J_STEP))
-            scalar_run, count = multiply_on_scalar(tiles, j0, pieces)
-            return tiles, scalar_run, count
+            return run
 
         def quantise_and_contract(tiles, groups, cuts=1):
             accs = {}
@@ -292,43 +244,88 @@ def tile_recon_loss_pa_t_kernel(tc, X, A, B, C_words, C_scales, out):
                         out=out[:, step * J_STEP + js.start : step * J_STEP + js.stop, :], in_=result[:]
                     )
 
-        def copy_sums(accs):
-            copies = []
-            for group in sorted(accs):
-                if group % COPIES == 0:
-                    copied = results.tile([P, COPIES * J_GROUP, N3], F32, name="copied", bufs=2 * GROUPS // COPIES)
-                    copies.append(copied)
-                first = (group % COPIES) * J_GROUP
-                nc.scalar.copy(out=copied[:, first : first + J_GROUP, :], in_=accs[group][:])
-            return copies
+        def copy_sums(accs, groups):
+            copied = results.tile([P, COPIES * J_GROUP, N3], F32, name="copied", bufs=2 * GROUPS // COPIES)
+            for n, group in enumerate(groups):
+                nc.scalar.copy(out=copied[:, n * J_GROUP : (n + 1) * J_GROUP, :], in_=accs[group][:])
+            return copied
 
-        def subtract_copied_and_store(step, copies):
-            width = COPIES * J_GROUP
-            for n, copied in enumerate(copies):
-                js = slice(n * width, (n + 1) * width)
-                nc.gpsimd.tensor_tensor(
-                    out=copied[:], in0=copied[:], in1=x_steps[step][:, js, :], op=mybir.AluOpType.subtract
-                )
-                first = step * J_STEP + js.start
-                nc.sync.dma_start(out=out[:, first : first + width, :], in_=copied[:])
+        def subtract_copied_and_store(step, groups, copied):
+            first, last = step * J_STEP + groups[0] * J_GROUP, step * J_STEP + (groups[-1] + 1) * J_GROUP
+            x = x_steps[step][:, groups[0] * J_GROUP : (groups[-1] + 1) * J_GROUP, :]
+            nc.gpsimd.tensor_tensor(out=copied[:], in0=copied[:], in1=x, op=mybir.AluOpType.subtract)
+            nc.sync.dma_start(out=out[:, first:last, :], in_=copied[:])
 
-        step_products, copied_sums = {}, {}
-        for step in range(N_STEPS):
-            step_products[step], scalar_run, count = multiply(step)
-            if step - 2 in copied_sums:
-                subtract_copied_and_store(step - 2, copied_sums[step - 2])
-            if step == 0:
-                scalar_run(0, count)
-                fronts = [shares(n)[0] for n in range(1, N_STEPS)]
-                convert_for_scalar(slice(1, N_STEPS), slice(min(fronts) // PASSES, J_STEP))
-                continue
+        tiles = product_tiles()
+        front, extra, gpsimd = shares(0)
+        pairs = sorted(scalar_pairs(0), key=lambda pair: pair % PASSES)
+        scalar_run = multiply_on_scalar(0, tiles, pairs)
+        now = slice(0, J_STEP)
+
+        def multiply_first(g, a_words, groups):
+            a_factor = a_words.bitcast(BF16).rearrange("p (n t) -> p n t", t=PACK)
+            values = (front - g + 1) // PASSES
+            for group in groups:
+                width = min(J_GROUP, values - group * J_GROUP)
+                if width > 0:
+                    js = slice(group * J_GROUP, group * J_GROUP + width)
+                    shape = [P, width, N1, PACK]
+                    nc.vector.tensor_tensor(
+                        out=tiles[group][:, 0:width, g],
+                        in0=bt[:, js, g].unsqueeze(2).to_broadcast(shape),
+                        in1=a_factor.unsqueeze(1).to_broadcast(shape),
+                        op=mybir.AluOpType.mult,
+                    )
+
+        for_vector = []
+        for g in range(PASSES):
+            b_words = turned_bank(b_rows[g]).rearrange("p (n h) -> p n h", h=HALVES)
+            nc.vector.tensor_copy(out=as_words(bt[:, now, g]), in_=b_words[:, now])
+            for_vector.append(turned_bank(a_rows[g]))
+            if g == 0:
+                multiply_first(0, for_vector[0], range(1))
+            nc.scalar.copy(out=at[:, g].rearrange("p n t -> p (n t)").bitcast(F32), in_=turned_bank(a_rows[g]))
+            convert_for_scalar(slice(0, 1), min(pairs), slice(g, g + 1))
+            if g == 0:
+                scalar_run(0, 1)
+        multiply_on_gpsimd(0, tiles)
+        multiply_first(0, for_vector[0], range(1, GROUPS))
+        b_bank = sums.tile([P, J_GROUP * N3], F32, name="acc")
+        for g in range(PASSES):
+            turn(b_rows[g], b_bank[:].rearrange("p (n g h) -> p n g h", g=PASSES, h=HALVES)[:, :, g])
+        for g in range(PASSES):
+            turn(a_rows[g], a_turned[:, g])
+        scalar_run(1, 2)
+        now_words = J_STEP * PASSES * HALVES
+        nc.scalar.copy(
+            out=bt[:].rearrange("p n g t -> p (n g t)").bitcast(F32)[:, now_words:], in_=b_bank[:, now_words:]
+        )
+        multiply_first(1, for_vector[1], range(GROUPS))
+        scalar_run(2, len(pairs))
+        convert_for_scalar(slice(1, N_STEPS), min(shares(n)[0] for n in range(1, N_STEPS)), slice(0, PASSES))
+
+        runs = [list(range(n, n + COPIES)) for n in range(0, GROUPS, COPIES)]
+        step_products, copied_sums, late = {0: tiles}, {}, []
+        for step in range(1, N_STEPS):
+            tiles = product_tiles()
+            step_products[step] = tiles
+            multiply_on_vector(step, tiles)
+            multiply_on_gpsimd(step, tiles)
+            for groups, copied in copied_sums.get(step - 2, []):
+                subtract_copied_and_store(step - 2, groups, copied)
+            pairs = scalar_pairs(step)
+            scalar_run = multiply_on_scalar(step, tiles, pairs)
             scalar_run(0, SCALAR_FIRST)
             accs = quantise_and_contract(step_products[step - 1], range(GROUPS))
             if subtracts_on_gpsimd(step - 1):
-                copied_sums[step - 1] = copy_sums(accs)
+                at_once = runs[:1] if step == N_STEPS - 2 else runs
+                copied_sums[step - 1] = [(groups, copy_sums(accs, groups)) for groups in at_once]
+                late = [(groups, accs) for groups in runs if groups not in at_once]
             else:
                 subtract_and_store(step - 1, accs)
-            scalar_run(SCALAR_FIRST, count)
+                for groups, accs in late:
+                    subtract_copied_and_store(step - 2, groups, copy_sums(accs, groups))
+            scalar_run(SCALAR_FIRST, len(pairs))
         last = step_products[N_STEPS - 1]
         early = quantise_and_contract(last, range(GROUPS - 1))
         subtract_and_store(N_STEPS - 1, {group: early[group] for group in range(GROUPS - 2)})

@@ -23,8 +23,7 @@ J_STEP = 16
 GROUPS = J_STEP // J_GROUP
 N_STEPS = N2 // J_STEP
 PAIRS_STEP = J_STEP * PASSES
-PAIRS_GROUP = J_GROUP * PASSES
-GPSIMD_GROUP = GROUPS - 2
+J_FRONT = J_STEP - J_GROUP
 
 
 def shares(step):
@@ -118,31 +117,34 @@ def tile_recon_loss_pa_t_kernel(tc, X, A, B, C_words, C_scales, out):
 
         def product_tiles():
             tiles = []
-            for group in range(GROUPS):
-                group_tile = products.tile(
-                    [P, J_GROUP, PASSES, N1, PACK], BF16, align_bytes=64, name="product%d" % group
-                )
-                tiles.append(group_tile)
+            for n, js in enumerate((J_FRONT, J_STEP - J_FRONT)):
+                tile = products.tile([P, js, PASSES, N1, PACK], BF16, align_bytes=64, name="product%d" % n)
+                tiles.append(tile)
             return tiles
 
-        def multiply_in_one_tile(engine, a_factor, product, j0, first, last):
+        def product_of(tiles, jl):
+            return (tiles[0], jl) if jl < J_FRONT else (tiles[1], jl - J_FRONT)
+
+        def multiply(engine, a_factor, tiles, j0, first, last):
             def one_pair(pair):
                 jl, g = pair // PASSES, pair % PASSES
+                product, place = product_of(tiles, jl)
                 engine.tensor_tensor(
-                    out=product[:, jl, g],
+                    out=product[:, place, g],
                     in0=bt[:, j0 + jl, g].unsqueeze(1).to_broadcast([P, N1, PACK]),
                     in1=a_factor[:, g],
                     op=mybir.AluOpType.mult,
                 )
 
-            if first % PASSES:
+            if first < last and first % PASSES:
                 one_pair(first)
                 first += 1
             jl, whole = first // PASSES, (last - first) // PASSES
             if whole:
                 shape = [P, whole, PASSES, N1, PACK]
+                product, place = product_of(tiles, jl)
                 engine.tensor_tensor(
-                    out=product[:, jl : jl + whole],
+                    out=product[:, place : place + whole],
                     in0=bt[:, j0 + jl : j0 + jl + whole].unsqueeze(3).to_broadcast(shape),
                     in1=a_factor.unsqueeze(1).to_broadcast(shape),
                     op=mybir.AluOpType.mult,
@@ -150,14 +152,7 @@ def tile_recon_loss_pa_t_kernel(tc, X, A, B, C_words, C_scales, out):
             if (last - first) % PASSES:
                 one_pair(last - 1)
 
-        def multiply(engine, a_factor, tiles, j0, first, last):
-            for group in range(GROUPS):
-                start = group * PAIRS_GROUP
-                low, high = max(first - start, 0), min(last - start, PAIRS_GROUP)
-                if low < high:
-                    multiply_in_one_tile(engine, a_factor, tiles[group], j0 + group * J_GROUP, low, high)
-
-        END_GPSIMD = (GPSIMD_GROUP + 1) * PAIRS_GROUP
+        END_GPSIMD = J_FRONT * PASSES
 
         def multiply_on_vector(step, tiles):
             front, extra, unused = shares(step)
@@ -176,7 +171,8 @@ def tile_recon_loss_pa_t_kernel(tc, X, A, B, C_words, C_scales, out):
 
             def group_words(n):
                 pair = pairs[n]
-                product = tiles[pair // PAIRS_GROUP][:, (pair // PASSES) % J_GROUP, pair % PASSES]
+                product, place = product_of(tiles, pair // PASSES)
+                product = product[:, place, pair % PASSES]
                 nc.scalar.copy(
                     out=product.rearrange("p i t -> p (i t)").bitcast(F32).rearrange("p (i h) -> p i h", h=HALVES),
                     in_=planes[:, n]
@@ -207,12 +203,13 @@ def tile_recon_loss_pa_t_kernel(tc, X, A, B, C_words, C_scales, out):
             for group in groups:
                 codes = quantised.tile([P, J_GROUP * PASSES * N1], U32, align_bytes=64, name="codes")
                 scales = quantised.tile([P, J_GROUP * PASSES * N1], U8, align_bytes=64, name="scales")
+                product, place = product_of(tiles, group * J_GROUP)
                 js, words = J_GROUP // cuts, J_GROUP * PASSES * N1 // cuts
                 for cut in range(cuts):
                     nc.vector.quantize_mx(
                         out=codes[:, cut * words : (cut + 1) * words].bitcast(FP8X4),
                         scales=scales[:, cut * words : (cut + 1) * words],
-                        in_=tiles[group][:, cut * js : (cut + 1) * js].rearrange("p j g i t -> p (j g i t)"),
+                        in_=product[:, place + cut * js : place + (cut + 1) * js].rearrange("p j g i t -> p (j g i t)"),
                     )
                 acc = sums.tile([P, J_GROUP, N3], F32, name="acc")
                 for jl in range(J_GROUP):
@@ -262,20 +259,15 @@ def tile_recon_loss_pa_t_kernel(tc, X, A, B, C_words, C_scales, out):
         scalar_run = multiply_on_scalar(0, tiles, pairs)
         now = slice(0, J_STEP)
 
-        def multiply_first(g, a_words, groups):
+        def multiply_first(g, a_words, first, last):
             a_factor = a_words.bitcast(BF16).rearrange("p (n t) -> p n t", t=PACK)
-            values = (front - g + 1) // PASSES
-            for group in groups:
-                width = min(J_GROUP, values - group * J_GROUP)
-                if width > 0:
-                    js = slice(group * J_GROUP, group * J_GROUP + width)
-                    shape = [P, width, N1, PACK]
-                    nc.vector.tensor_tensor(
-                        out=tiles[group][:, 0:width, g],
-                        in0=bt[:, js, g].unsqueeze(2).to_broadcast(shape),
-                        in1=a_factor.unsqueeze(1).to_broadcast(shape),
-                        op=mybir.AluOpType.mult,
-                    )
+            shape = [P, last - first, N1, PACK]
+            nc.vector.tensor_tensor(
+                out=tiles[0][:, first:last, g],
+                in0=bt[:, first:last, g].unsqueeze(2).to_broadcast(shape),
+                in1=a_factor.unsqueeze(1).to_broadcast(shape),
+                op=mybir.AluOpType.mult,
+            )
 
         for_vector = []
         for g in range(PASSES):
@@ -283,13 +275,13 @@ def tile_recon_loss_pa_t_kernel(tc, X, A, B, C_words, C_scales, out):
             nc.vector.tensor_copy(out=as_words(bt[:, now, g]), in_=b_words[:, now])
             for_vector.append(turned_bank(a_rows[g]))
             if g == 0:
-                multiply_first(0, for_vector[0], range(1))
+                multiply_first(0, for_vector[0], 0, J_GROUP)
             nc.scalar.copy(out=at[:, g].rearrange("p n t -> p (n t)").bitcast(F32), in_=turned_bank(a_rows[g]))
             convert_for_scalar(slice(0, 1), min(pairs), slice(g, g + 1))
             if g == 0:
                 scalar_run(0, 1)
         multiply_on_gpsimd(0, tiles)
-        multiply_first(0, for_vector[0], range(1, GROUPS))
+        multiply_first(0, for_vector[0], J_GROUP, front // PASSES)
         b_bank = sums.tile([P, J_GROUP * N3], F32, name="acc")
         for g in range(PASSES):
             turn(b_rows[g], b_bank[:].rearrange("p (n g h) -> p n g h", g=PASSES, h=HALVES)[:, :, g])
@@ -300,7 +292,7 @@ def tile_recon_loss_pa_t_kernel(tc, X, A, B, C_words, C_scales, out):
         nc.scalar.copy(
             out=bt[:].rearrange("p n g t -> p (n g t)").bitcast(F32)[:, now_words:], in_=b_bank[:, now_words:]
         )
-        multiply_first(1, for_vector[1], range(GROUPS))
+        multiply_first(1, for_vector[1], 0, front // PASSES)
         scalar_run(2, len(pairs))
         convert_for_scalar(slice(1, N_STEPS), min(shares(n)[0] for n in range(1, N_STEPS)), slice(0, PASSES))
 

@@ -31,13 +31,14 @@ def shares(step):
         return 20, 0, 4
     if step == N_STEPS - 1:
         return 20, 0, 2
-    return 23, (step + 1) % 2, 1
+    return 22, (step + 1) % 2, 0
 
 
 def subtracts_on_gpsimd(step):
     return step < N_STEPS - 2
 
 
+SHARED_ROWS = 48
 COPIES = 2
 SCALAR_FIRST = 4
 
@@ -154,17 +155,34 @@ def tile_recon_loss_pa_t_kernel(tc, X, A, B, C_words, C_scales, out):
 
         END_GPSIMD = J_FRONT * PASSES
 
+        def is_shared(step):
+            return shares(step)[2] == 0
+
+        def multiply_rows(engine, a_factor, step, tiles, rows):
+            shape = [P, PASSES, rows.stop - rows.start, PACK]
+            engine.tensor_tensor(
+                out=tiles[0][:, J_FRONT - 1, :, rows],
+                in0=bt[:, step * J_STEP + J_FRONT - 1].unsqueeze(2).to_broadcast(shape),
+                in1=a_factor[:, :, rows],
+                op=mybir.AluOpType.mult,
+            )
+
         def multiply_on_vector(step, tiles):
             front, extra, unused = shares(step)
             multiply(nc.vector, at_in_psum, tiles, step * J_STEP, 0, front)
             multiply(nc.vector, at_in_psum, tiles, step * J_STEP, END_GPSIMD, END_GPSIMD + extra)
+            if is_shared(step):
+                multiply_rows(nc.vector, at_in_psum, step, tiles, slice(0, SHARED_ROWS))
 
         def multiply_on_gpsimd(step, tiles):
+            if is_shared(step):
+                multiply_rows(nc.gpsimd, at[:], step, tiles, slice(SHARED_ROWS, N1))
             multiply(nc.gpsimd, at[:], tiles, step * J_STEP, END_GPSIMD - shares(step)[2], END_GPSIMD)
 
         def scalar_pairs(step):
             front, extra, gpsimd = shares(step)
-            return list(range(front, END_GPSIMD - gpsimd)) + list(range(END_GPSIMD + extra, PAIRS_STEP))
+            end = END_GPSIMD - (PASSES if is_shared(step) else gpsimd)
+            return list(range(front, end)) + list(range(END_GPSIMD + extra, PAIRS_STEP))
 
         def multiply_on_scalar(step, tiles, pairs):
             planes = products.tile([P, len(pairs), HALVES, N1, PACK // HALVES], BF16, name="planes")

@@ -27,18 +27,19 @@ J_FRONT = J_STEP - J_GROUP
 
 
 def shares(step):
-    if step < 2:
-        return 20, 0, 4
+    if step == 0:
+        return 20, 0, 2, 0
+    if step == 1:
+        return 18, 0, 3, 32
     if step == N_STEPS - 1:
-        return 20, 0, 2
-    return 22, (step + 1) % 2, 0
+        return 20, 0, 1, 0
+    return 22, (step + 1) % 2, 1, 48
 
 
 def subtracts_on_gpsimd(step):
     return step < N_STEPS - 2
 
 
-SHARED_ROWS = 48
 COPIES = 2
 SCALAR_FIRST = 4
 
@@ -155,49 +156,52 @@ def tile_recon_loss_pa_t_kernel(tc, X, A, B, C_words, C_scales, out):
 
         END_GPSIMD = J_FRONT * PASSES
 
-        def is_shared(step):
-            return shares(step)[2] == 0
-
         def multiply_rows(engine, a_factor, step, tiles, rows):
-            shape = [P, PASSES, rows.stop - rows.start, PACK]
+            if rows.start == rows.stop:
+                return
+            count = shares(step)[2]
+            js = slice(J_FRONT - count, J_FRONT)
+            shape = [P, count, PASSES, rows.stop - rows.start, PACK]
             engine.tensor_tensor(
-                out=tiles[0][:, J_FRONT - 1, :, rows],
-                in0=bt[:, step * J_STEP + J_FRONT - 1].unsqueeze(2).to_broadcast(shape),
-                in1=a_factor[:, :, rows],
+                out=tiles[0][:, js, :, rows],
+                in0=bt[:, step * J_STEP + js.start : step * J_STEP + js.stop].unsqueeze(3).to_broadcast(shape),
+                in1=a_factor[:, :, rows].unsqueeze(1).to_broadcast(shape),
                 op=mybir.AluOpType.mult,
             )
 
         def multiply_on_vector(step, tiles):
-            front, extra, unused = shares(step)
+            front, extra, unused, rows = shares(step)
             multiply(nc.vector, at_in_psum, tiles, step * J_STEP, 0, front)
             multiply(nc.vector, at_in_psum, tiles, step * J_STEP, END_GPSIMD, END_GPSIMD + extra)
-            if is_shared(step):
-                multiply_rows(nc.vector, at_in_psum, step, tiles, slice(0, SHARED_ROWS))
+            multiply_rows(nc.vector, at_in_psum, step, tiles, slice(0, rows))
 
         def multiply_on_gpsimd(step, tiles):
-            if is_shared(step):
-                multiply_rows(nc.gpsimd, at[:], step, tiles, slice(SHARED_ROWS, N1))
-            multiply(nc.gpsimd, at[:], tiles, step * J_STEP, END_GPSIMD - shares(step)[2], END_GPSIMD)
+            multiply_rows(nc.gpsimd, at[:], step, tiles, slice(shares(step)[3], N1))
 
         def scalar_pairs(step):
-            front, extra, gpsimd = shares(step)
-            end = END_GPSIMD - (PASSES if is_shared(step) else gpsimd)
-            return list(range(front, end)) + list(range(END_GPSIMD + extra, PAIRS_STEP))
+            front, extra, values, unused = shares(step)
+            return list(range(front, END_GPSIMD - values * PASSES)) + list(range(END_GPSIMD + extra, PAIRS_STEP))
 
         def multiply_on_scalar(step, tiles, pairs):
             planes = products.tile([P, len(pairs), HALVES, N1, PACK // HALVES], BF16, name="planes")
 
-            def group_words(n):
-                pair = pairs[n]
-                product, place = product_of(tiles, pair // PASSES)
-                product = product[:, place, pair % PASSES]
+            def group_words(first, last):
+                product, place = product_of(tiles, pairs[first] // PASSES)
+                start = place * PASSES + pairs[first] % PASSES
+                product = product[:].rearrange("p j g i t -> p (j g) (i t)")[:, start : start + last - first]
                 nc.scalar.copy(
-                    out=product.rearrange("p i t -> p (i t)").bitcast(F32).rearrange("p (i h) -> p i h", h=HALVES),
-                    in_=planes[:, n]
-                    .rearrange("p h i e -> p h (i e)")
+                    out=product.bitcast(F32).rearrange("p n (i h) -> p n i h", h=HALVES),
+                    in_=planes[:, first:last]
+                    .rearrange("p n h i e -> p n h (i e)")
                     .bitcast(F32)
-                    .rearrange("p h i -> p i h"),
+                    .rearrange("p n h i -> p n i h"),
                 )
+
+            ends = [
+                n
+                for n in range(1, len(pairs) + 1)
+                if n == len(pairs) or pairs[n] % PASSES == 0 or pairs[n] != pairs[n - 1] + 1
+            ]
 
             def run(low, high):
                 for n in range(low, high):
@@ -209,10 +213,10 @@ def tile_recon_loss_pa_t_kernel(tc, X, A, B, C_words, C_scales, out):
                             func=mybir.ActivationFunctionType.Copy,
                             scale=bt_f32[:, j, g, t : t + 1],
                         )
-                    if n > 0:
-                        group_words(n - 1)
+                    if n in ends:
+                        group_words(max([0] + [end for end in ends if end < n]), n)
                 if high == len(pairs):
-                    group_words(high - 1)
+                    group_words(max([0] + [end for end in ends if end < high]), high)
 
             return run
 
@@ -272,15 +276,14 @@ def tile_recon_loss_pa_t_kernel(tc, X, A, B, C_words, C_scales, out):
             nc.sync.dma_start(out=out[:, first:last, :], in_=copied[:])
 
         tiles = product_tiles()
-        front, extra, gpsimd = shares(0)
+        front, unused, gpsimd_values, unused = shares(0)
         pairs = sorted(scalar_pairs(0), key=lambda pair: pair % PASSES)
         scalar_run = multiply_on_scalar(0, tiles, pairs)
         now = slice(0, J_STEP)
 
-        def multiply_first(g, a_words, first, last):
-            a_factor = a_words.bitcast(BF16).rearrange("p (n t) -> p n t", t=PACK)
+        def multiply_first(engine, g, a_factor, first, last):
             shape = [P, last - first, N1, PACK]
-            nc.vector.tensor_tensor(
+            engine.tensor_tensor(
                 out=tiles[0][:, first:last, g],
                 in0=bt[:, first:last, g].unsqueeze(2).to_broadcast(shape),
                 in1=a_factor.unsqueeze(1).to_broadcast(shape),
@@ -291,15 +294,15 @@ def tile_recon_loss_pa_t_kernel(tc, X, A, B, C_words, C_scales, out):
         for g in range(PASSES):
             b_words = turned_bank(b_rows[g]).rearrange("p (n h) -> p n h", h=HALVES)
             nc.vector.tensor_copy(out=as_words(bt[:, now, g]), in_=b_words[:, now])
-            for_vector.append(turned_bank(a_rows[g]))
+            for_vector.append(turned_bank(a_rows[g]).bitcast(BF16).rearrange("p (n t) -> p n t", t=PACK))
             if g == 0:
-                multiply_first(0, for_vector[0], 0, J_GROUP)
+                multiply_first(nc.vector, 0, for_vector[0], 0, J_GROUP)
             nc.scalar.copy(out=at[:, g].rearrange("p n t -> p (n t)").bitcast(F32), in_=turned_bank(a_rows[g]))
+            multiply_first(nc.gpsimd, g, at[:, g], J_FRONT - gpsimd_values, J_FRONT)
             convert_for_scalar(slice(0, 1), min(pairs), slice(g, g + 1))
             if g == 0:
                 scalar_run(0, 1)
-        multiply_on_gpsimd(0, tiles)
-        multiply_first(0, for_vector[0], J_GROUP, front // PASSES)
+        multiply_first(nc.vector, 0, for_vector[0], J_GROUP, front // PASSES)
         b_bank = sums.tile([P, J_GROUP * N3], F32, name="acc")
         for g in range(PASSES):
             turn(b_rows[g], b_bank[:].rearrange("p (n g h) -> p n g h", g=PASSES, h=HALVES)[:, :, g])
@@ -310,9 +313,9 @@ def tile_recon_loss_pa_t_kernel(tc, X, A, B, C_words, C_scales, out):
         nc.scalar.copy(
             out=bt[:].rearrange("p n g t -> p (n g t)").bitcast(F32)[:, now_words:], in_=b_bank[:, now_words:]
         )
-        multiply_first(1, for_vector[1], 0, front // PASSES)
+        multiply_first(nc.vector, 1, for_vector[1], 0, front // PASSES)
         scalar_run(2, len(pairs))
-        convert_for_scalar(slice(1, N_STEPS), min(shares(n)[0] for n in range(1, N_STEPS)), slice(0, PASSES))
+        convert_for_scalar(slice(1, N_STEPS), min(scalar_pairs(n)[0] for n in range(1, N_STEPS)), slice(0, PASSES))
 
         runs = [list(range(n, n + COPIES)) for n in range(0, GROUPS, COPIES)]
         step_products, copied_sums, late = {0: tiles}, {}, []

@@ -94,8 +94,8 @@ def tile_recon_loss_pa_t_kernel(tc, X, A, B, C_words, C_scales, out):
         bt = keep.tile([P, N2, PASSES, PACK], BF16)
         at = keep.tile([P, PASSES, N1, PACK], BF16)
         bt_f32 = keep.tile([P, N2, PASSES, PACK], F32)
-        a_turned = turned.tile([P, PASSES, N1, HALVES], F32)
-        at_in_psum = a_turned[:].bitcast(BF16)
+        b_turned = turned.tile([P, N2, PASSES, HALVES], F32)
+        bt_in_psum = b_turned[:].bitcast(BF16)
 
         def turn(rows, words_out):
             for h in range(HALVES):
@@ -110,11 +110,11 @@ def tile_recon_loss_pa_t_kernel(tc, X, A, B, C_words, C_scales, out):
         def as_words(factor):
             return factor.bitcast(F32)
 
-        def convert_for_scalar(steps, first_pair, passes):
+        def convert_for_scalar(b_factor, steps, first_pair, passes):
             js = slice(first_pair // PASSES, J_STEP)
             nc.scalar.copy(
                 out=bt_f32[:].rearrange("p (s j) g t -> p s j g t", j=J_STEP)[:, steps, js, passes],
-                in_=bt[:].rearrange("p (s j) g t -> p s j g t", j=J_STEP)[:, steps, js, passes],
+                in_=b_factor.rearrange("p (s j) g t -> p s j g t", j=J_STEP)[:, steps, js, passes],
             )
 
         def product_tiles():
@@ -127,14 +127,14 @@ def tile_recon_loss_pa_t_kernel(tc, X, A, B, C_words, C_scales, out):
         def product_of(tiles, jl):
             return (tiles[0], jl) if jl < J_FRONT else (tiles[1], jl - J_FRONT)
 
-        def multiply(engine, a_factor, tiles, j0, first, last):
+        def multiply_on_vector_pairs(tiles, j0, first, last):
             def one_pair(pair):
                 jl, g = pair // PASSES, pair % PASSES
                 product, place = product_of(tiles, jl)
-                engine.tensor_tensor(
+                nc.vector.tensor_tensor(
                     out=product[:, place, g],
-                    in0=bt[:, j0 + jl, g].unsqueeze(1).to_broadcast([P, N1, PACK]),
-                    in1=a_factor[:, g],
+                    in0=bt_in_psum[:, j0 + jl, g].unsqueeze(1).to_broadcast([P, N1, PACK]),
+                    in1=at[:, g],
                     op=mybir.AluOpType.mult,
                 )
 
@@ -145,10 +145,10 @@ def tile_recon_loss_pa_t_kernel(tc, X, A, B, C_words, C_scales, out):
             if whole:
                 shape = [P, whole, PASSES, N1, PACK]
                 product, place = product_of(tiles, jl)
-                engine.tensor_tensor(
+                nc.vector.tensor_tensor(
                     out=product[:, place : place + whole],
-                    in0=bt[:, j0 + jl : j0 + jl + whole].unsqueeze(3).to_broadcast(shape),
-                    in1=a_factor.unsqueeze(1).to_broadcast(shape),
+                    in0=bt_in_psum[:, j0 + jl : j0 + jl + whole].unsqueeze(3).to_broadcast(shape),
+                    in1=at[:].unsqueeze(1).to_broadcast(shape),
                     op=mybir.AluOpType.mult,
                 )
             if (last - first) % PASSES:
@@ -156,7 +156,7 @@ def tile_recon_loss_pa_t_kernel(tc, X, A, B, C_words, C_scales, out):
 
         END_GPSIMD = J_FRONT * PASSES
 
-        def multiply_rows(engine, a_factor, step, tiles, rows):
+        def multiply_rows(engine, b_factor, step, tiles, rows):
             if rows.start == rows.stop:
                 return
             count = shares(step)[2]
@@ -164,19 +164,19 @@ def tile_recon_loss_pa_t_kernel(tc, X, A, B, C_words, C_scales, out):
             shape = [P, count, PASSES, rows.stop - rows.start, PACK]
             engine.tensor_tensor(
                 out=tiles[0][:, js, :, rows],
-                in0=bt[:, step * J_STEP + js.start : step * J_STEP + js.stop].unsqueeze(3).to_broadcast(shape),
-                in1=a_factor[:, :, rows].unsqueeze(1).to_broadcast(shape),
+                in0=b_factor[:, step * J_STEP + js.start : step * J_STEP + js.stop].unsqueeze(3).to_broadcast(shape),
+                in1=at[:, :, rows].unsqueeze(1).to_broadcast(shape),
                 op=mybir.AluOpType.mult,
             )
 
         def multiply_on_vector(step, tiles):
             front, extra, unused, rows = shares(step)
-            multiply(nc.vector, at_in_psum, tiles, step * J_STEP, 0, front)
-            multiply(nc.vector, at_in_psum, tiles, step * J_STEP, END_GPSIMD, END_GPSIMD + extra)
-            multiply_rows(nc.vector, at_in_psum, step, tiles, slice(0, rows))
+            multiply_on_vector_pairs(tiles, step * J_STEP, 0, front)
+            multiply_on_vector_pairs(tiles, step * J_STEP, END_GPSIMD, END_GPSIMD + extra)
+            multiply_rows(nc.vector, bt_in_psum, step, tiles, slice(0, rows))
 
         def multiply_on_gpsimd(step, tiles):
-            multiply_rows(nc.gpsimd, at[:], step, tiles, slice(shares(step)[3], N1))
+            multiply_rows(nc.gpsimd, bt[:], step, tiles, slice(shares(step)[3], N1))
 
         def scalar_pairs(step):
             front, extra, values, unused = shares(step)
@@ -185,23 +185,17 @@ def tile_recon_loss_pa_t_kernel(tc, X, A, B, C_words, C_scales, out):
         def multiply_on_scalar(step, tiles, pairs):
             planes = products.tile([P, len(pairs), HALVES, N1, PACK // HALVES], BF16, name="planes")
 
-            def group_words(first, last):
-                product, place = product_of(tiles, pairs[first] // PASSES)
-                start = place * PASSES + pairs[first] % PASSES
-                product = product[:].rearrange("p j g i t -> p (j g) (i t)")[:, start : start + last - first]
+            def group_words(n):
+                pair = pairs[n]
+                product, place = product_of(tiles, pair // PASSES)
+                product = product[:, place, pair % PASSES]
                 nc.scalar.copy(
-                    out=product.bitcast(F32).rearrange("p n (i h) -> p n i h", h=HALVES),
-                    in_=planes[:, first:last]
-                    .rearrange("p n h i e -> p n h (i e)")
+                    out=product.rearrange("p i t -> p (i t)").bitcast(F32).rearrange("p (i h) -> p i h", h=HALVES),
+                    in_=planes[:, n]
+                    .rearrange("p h i e -> p h (i e)")
                     .bitcast(F32)
-                    .rearrange("p n h i -> p n i h"),
+                    .rearrange("p h i -> p i h"),
                 )
-
-            ends = [
-                n
-                for n in range(1, len(pairs) + 1)
-                if n == len(pairs) or pairs[n] % PASSES == 0 or pairs[n] != pairs[n - 1] + 1
-            ]
 
             def run(low, high):
                 for n in range(low, high):
@@ -213,10 +207,10 @@ def tile_recon_loss_pa_t_kernel(tc, X, A, B, C_words, C_scales, out):
                             func=mybir.ActivationFunctionType.Copy,
                             scale=bt_f32[:, j, g, t : t + 1],
                         )
-                    if n in ends:
-                        group_words(max([0] + [end for end in ends if end < n]), n)
+                    if n > 0:
+                        group_words(n - 1)
                 if high == len(pairs):
-                    group_words(max([0] + [end for end in ends if end < high]), high)
+                    group_words(high - 1)
 
             return run
 
@@ -299,23 +293,21 @@ def tile_recon_loss_pa_t_kernel(tc, X, A, B, C_words, C_scales, out):
                 multiply_first(nc.vector, 0, for_vector[0], 0, J_GROUP)
             nc.scalar.copy(out=at[:, g].rearrange("p n t -> p (n t)").bitcast(F32), in_=turned_bank(a_rows[g]))
             multiply_first(nc.gpsimd, g, at[:, g], J_FRONT - gpsimd_values, J_FRONT)
-            convert_for_scalar(slice(0, 1), min(pairs), slice(g, g + 1))
+            convert_for_scalar(bt[:], slice(0, 1), min(pairs), slice(g, g + 1))
             if g == 0:
                 scalar_run(0, 1)
         multiply_first(nc.vector, 0, for_vector[0], J_GROUP, front // PASSES)
-        b_bank = sums.tile([P, J_GROUP * N3], F32, name="acc")
         for g in range(PASSES):
-            turn(b_rows[g], b_bank[:].rearrange("p (n g h) -> p n g h", g=PASSES, h=HALVES)[:, :, g])
-        for g in range(PASSES):
-            turn(a_rows[g], a_turned[:, g])
+            turn(b_rows[g], b_turned[:, :, g])
         scalar_run(1, 2)
-        now_words = J_STEP * PASSES * HALVES
+        own = slice(J_FRONT - max(shares(n)[2] for n in range(1, N_STEPS)), J_FRONT)
         nc.scalar.copy(
-            out=bt[:].rearrange("p n g t -> p (n g t)").bitcast(F32)[:, now_words:], in_=b_bank[:, now_words:]
+            out=bt[:].rearrange("p (s j) g t -> p s j (g t)", j=J_STEP)[:, 1:, own].bitcast(F32),
+            in_=b_turned[:].rearrange("p (s j) g h -> p s j (g h)", j=J_STEP)[:, 1:, own],
         )
+        convert_for_scalar(bt_in_psum, slice(1, N_STEPS), min(scalar_pairs(n)[0] for n in range(1, N_STEPS)), slice(0, PASSES))
         multiply_first(nc.vector, 1, for_vector[1], 0, front // PASSES)
         scalar_run(2, len(pairs))
-        convert_for_scalar(slice(1, N_STEPS), min(scalar_pairs(n)[0] for n in range(1, N_STEPS)), slice(0, PASSES))
 
         runs = [list(range(n, n + COPIES)) for n in range(0, GROUPS, COPIES)]
         step_products, copied_sums, late = {0: tiles}, {}, []

from contextlib import ExitStack

import concourse.mybir as mybir
from concourse.masks import make_identity

F32 = mybir.dt.float32
BF16 = mybir.dt.bfloat16
I32 = mybir.dt.int32
U32 = mybir.dt.uint32
U8 = mybir.dt.uint8
FP8X4 = mybir.dt.float8_e4m3fn_x4
FP4X4 = mybir.dt.float4_e2m1fn_x4

P = 128
PACK = 4
N1, N2, N3, R = 128, 128, 128, 1024
PASSES = R // (P * PACK)
WORDS = R // 2
HALVES = PACK // 2

J_GROUP = 4
J_STEP = 16
GROUPS = J_STEP // J_GROUP
N_STEPS = N2 // J_STEP
PAIRS_STEP = J_STEP * PASSES
J_FRONT = J_STEP - J_GROUP


def shares(step):
    if step == 0:
        return 20, 0, 2, 0
    if step == 1:
        return 18, 0, 3, 32
    if step == N_STEPS - 1:
        return 20, 0, 1, 0
    return 22, (step + 1) % 2, 1, 48


def subtracts_on_gpsimd(step):
    return step < N_STEPS - 2


COPIES = 2
SCALAR_FIRST = 4

FLOPS = 2 * N1 * N2 * N3 * R


def tile_recon_loss_pa_t_kernel(tc, X, A, B, C_words, C_scales, out):
    nc = tc.nc

    with ExitStack() as stack:
        stack.enter_context(tc.manual_schedule())
        keep = stack.enter_context(tc.tile_pool(name="keep", bufs=1))
        products = stack.enter_context(tc.tile_pool(name="products", bufs=2))
        quantised = stack.enter_context(tc.tile_pool(name="quantised", bufs=GROUPS + 1))
        results = stack.enter_context(tc.tile_pool(name="results", bufs=GROUPS + 2))
        turned = stack.enter_context(tc.psum_pool(name="turned", bufs=1))
        sums = stack.enter_context(tc.psum_pool(name="sums", bufs=7))

        w_scales = keep.tile([P, PASSES, N3], U8, align_bytes=64)
        nc.vector.memset(w_scales[:].bitcast(I32), 0)

        a_rows, b_rows = [], []
        for g in range(PASSES):
            half = slice(g * (R // PASSES), (g + 1) * (R // PASSES))
            b_piece = keep.tile([N2, R // PASSES], BF16, name="b_rows%d" % g)
            nc.sync.dma_start(out=b_piece[:], in_=B[:, half])
            b_rows.append(b_piece)
            a_piece = keep.tile([N1, R // PASSES], BF16, name="a_rows%d" % g)
            nc.scalar.dma_start(out=a_piece[:], in_=A[:, half])
            a_rows.append(a_piece)

        w_words = keep.tile([P, PASSES, 2 * N3], U8, align_bytes=64)
        nc.sync.dma_start(
            out=w_words[:].bitcast(I32), in_=C_words.bitcast(I32).rearrange("g p w -> p g w")
        )
        for quadrant in range(4):
            nc.sync.dma_start(
                out=w_scales[32 * quadrant : 32 * quadrant + 4].bitcast(I32),
                in_=C_scales.bitcast(I32)[:, 4 * quadrant : 4 * quadrant + 4, :].rearrange(
                    "g q w -> q g w"
                ),
            )

        x_steps = []
        for step in range(N_STEPS):
            x_step = keep.tile([N1, J_STEP, N3], BF16, name="x_step%d" % step)
            nc.sync.dma_start(out=x_step[:], in_=X[:, step * J_STEP : (step + 1) * J_STEP, :])
            x_steps.append(x_step)

        identity = keep.tile([P, P], F32)
        make_identity(nc, identity[:])
        bt = keep.tile([P, N2, PASSES, PACK], BF16)
        at = keep.tile([P, PASSES, N1, PACK], BF16)
        bt_f32 = keep.tile([P, N2, PASSES, PACK], F32)
        b_turned = turned.tile([P, N2, PASSES, HALVES], F32)
        bt_in_psum = b_turned[:].bitcast(BF16)

        def turn(rows, words_out):
            for h in range(HALVES):
                nc.tensor.transpose(words_out[:, :, h], rows[:].bitcast(F32)[:, h::HALVES], identity[:])

        def turned_bank(rows):
            bank = sums.tile([P, J_GROUP * N3], F32, name="acc")
            words = bank[:, 0 : N1 * HALVES]
            turn(rows, words.rearrange("p (n h) -> p n h", h=HALVES))
            return words

        def as_words(factor):
            return factor.bitcast(F32)

        def convert_for_scalar(b_factor, steps, first_pair, passes):
            js = slice(first_pair // PASSES, J_STEP)
            nc.scalar.copy(
                out=bt_f32[:].rearrange("p (s j) g t -> p s j g t", j=J_STEP)[:, steps, js, passes],
                in_=b_factor.rearrange("p (s j) g t -> p s j g t", j=J_STEP)[:, steps, js, passes],
            )

        def product_tiles():
            tiles = []
            for n, js in enumerate((J_FRONT, J_STEP - J_FRONT)):
                tile = products.tile([P, js, PASSES, N1, PACK], BF16, align_bytes=64, name="product%d" % n)
                tiles.append(tile)
            return tiles

        def product_of(tiles, jl):
            return (tiles[0], jl) if jl < J_FRONT else (tiles[1], jl - J_FRONT)

        def multiply_on_vector_pairs(tiles, j0, first, last):
            def one_pair(pair):
                jl, g = pair // PASSES, pair % PASSES
                product, place = product_of(tiles, jl)
                nc.vector.tensor_tensor(
                    out=product[:, place, g],
                    in0=bt_in_psum[:, j0 + jl, g].unsqueeze(1).to_broadcast([P, N1, PACK]),
                    in1=at[:, g],
                    op=mybir.AluOpType.mult,
                )

            if first < last and first % PASSES:
                one_pair(first)
                first += 1
            jl, whole = first // PASSES, (last - first) // PASSES
            if whole:
                shape = [P, whole, PASSES, N1, PACK]
                product, place = product_of(tiles, jl)
                nc.vector.tensor_tensor(
                    out=product[:, place : place + whole],
                    in0=bt_in_psum[:, j0 + jl : j0 + jl + whole].unsqueeze(3).to_broadcast(shape),
                    in1=at[:].unsqueeze(1).to_broadcast(shape),
                    op=mybir.AluOpType.mult,
                )
            if (last - first) % PASSES:
                one_pair(last - 1)

        END_GPSIMD = J_FRONT * PASSES

        def multiply_rows(engine, b_factor, step, tiles, rows):
            if rows.start == rows.stop:
                return
            count = shares(step)[2]
            js = slice(J_FRONT - count, J_FRONT)
            shape = [P, count, PASSES, rows.stop - rows.start, PACK]
            engine.tensor_tensor(
                out=tiles[0][:, js, :, rows],
                in0=b_factor[:, step * J_STEP + js.start : step * J_STEP + js.stop].unsqueeze(3).to_broadcast(shape),
                in1=at[:, :, rows].unsqueeze(1).to_broadcast(shape),
                op=mybir.AluOpType.mult,
            )

        def multiply_on_vector(step, tiles):
            front, extra, unused, rows = shares(step)
            multiply_on_vector_pairs(tiles, step * J_STEP, 0, front)
            multiply_on_vector_pairs(tiles, step * J_STEP, END_GPSIMD, END_GPSIMD + extra)
            multiply_rows(nc.vector, bt_in_psum, step, tiles, slice(0, rows))

        def multiply_on_gpsimd(step, tiles):
            multiply_rows(nc.gpsimd, bt[:], step, tiles, slice(shares(step)[3], N1))

        def scalar_pairs(step):
            front, extra, values, unused = shares(step)
            return list(range(front, END_GPSIMD - values * PASSES)) + list(range(END_GPSIMD + extra, PAIRS_STEP))

        def multiply_on_scalar(step, tiles, pairs):
            planes = products.tile([P, len(pairs), HALVES, N1, PACK // HALVES], BF16, name="planes")

            def group_words(n):
                pair = pairs[n]
                product, place = product_of(tiles, pair // PASSES)
                product = product[:, place, pair % PASSES]
                nc.scalar.copy(
                    out=product.rearrange("p i t -> p (i t)").bitcast(F32).rearrange("p (i h) -> p i h", h=HALVES),
                    in_=planes[:, n]
                    .rearrange("p h i e -> p h (i e)")
                    .bitcast(F32)
                    .rearrange("p h i -> p i h"),
                )

            def run(low, high):
                for n in range(low, high):
                    j, g = step * J_STEP + pairs[n] // PASSES, pairs[n] % PASSES
                    for t in range(PACK):
                        nc.scalar.activation(
                            out=planes[:, n, t // HALVES, :, t % HALVES],
                            in_=at[:, g, :, t],
                            func=mybir.ActivationFunctionType.Copy,
                            scale=bt_f32[:, j, g, t : t + 1],
                        )
                    if n > 0:
                        group_words(n - 1)
                if high == len(pairs):
                    group_words(high - 1)

            return run

        def quantise_and_contract(tiles, groups, cuts=1):
            accs = {}
            for group in groups:
                codes = quantised.tile([P, J_GROUP * PASSES * N1], U32, align_bytes=64, name="codes")
                scales = quantised.tile([P, J_GROUP * PASSES * N1], U8, align_bytes=64, name="scales")
                product, place = product_of(tiles, group * J_GROUP)
                js, words = J_GROUP // cuts, J_GROUP * PASSES * N1 // cuts
                for cut in range(cuts):
                    nc.vector.quantize_mx(
                        out=codes[:, cut * words : (cut + 1) * words].bitcast(FP8X4),
                        scales=scales[:, cut * words : (cut + 1) * words],
                        in_=product[:, place + cut * js : place + (cut + 1) * js].rearrange("p j g i t -> p (j g i t)"),
                    )
                acc = sums.tile([P, J_GROUP, N3], F32, name="acc")
                for jl in range(J_GROUP):
                    for g in range(PASSES):
                        first = (jl * PASSES + g) * N1
                        nc.tensor.matmul_mx(
                            out=acc[:, jl, :],
                            lhsT=codes[:, first : first + N1].bitcast(FP8X4),
                            lhsT_scale=scales[:, first : first + N1],
                            rhs=w_words[:, g, :].bitcast(FP4X4),
                            rhs_scale=w_scales[:, g, :],
                            start=(g == 0),
                            stop=(g == PASSES - 1),
                        )
                accs[group] = acc
            return accs

        def subtract_and_store(step, accs, cuts=1):
            width = J_GROUP // cuts
            for group in sorted(accs):
                for cut in range(cuts):
                    own = slice(cut * width, (cut + 1) * width)
                    js = slice(group * J_GROUP + own.start, group * J_GROUP + own.stop)
                    result = results.tile([P, width, N3], F32, name="result")
                    nc.vector.tensor_tensor(
                        out=result[:], in0=accs[group][:, own], in1=x_steps[step][:, js, :], op=mybir.AluOpType.subtract
                    )
                    nc.sync.dma_start(
                        out=out[:, step * J_STEP + js.start : step * J_STEP + js.stop, :], in_=result[:]
                    )

        def copy_sums(accs, groups):
            copied = results.tile([P, COPIES * J_GROUP, N3], F32, name="copied", bufs=2 * GROUPS // COPIES)
            for n, group in enumerate(groups):
                nc.scalar.copy(out=copied[:, n * J_GROUP : (n + 1) * J_GROUP, :], in_=accs[group][:])
            return copied

        def subtract_copied_and_store(step, groups, copied):
            first, last = step * J_STEP + groups[0] * J_GROUP, step * J_STEP + (groups[-1] + 1) * J_GROUP
            x = x_steps[step][:, groups[0] * J_GROUP : (groups[-1] + 1) * J_GROUP, :]
            nc.gpsimd.tensor_tensor(out=copied[:], in0=copied[:], in1=x, op=mybir.AluOpType.subtract)
            nc.sync.dma_start(out=out[:, first:last, :], in_=copied[:])

        tiles = product_tiles()
        front, unused, gpsimd_values, unused = shares(0)
        pairs = sorted(scalar_pairs(0), key=lambda pair: pair % PASSES)
        scalar_run = multiply_on_scalar(0, tiles, pairs)
        now = slice(0, J_STEP)

        def multiply_first(engine, g, a_factor, first, last):
            shape = [P, last - first, N1, PACK]
            engine.tensor_tensor(
                out=tiles[0][:, first:last, g],
                in0=bt[:, first:last, g].unsqueeze(2).to_broadcast(shape),
                in1=a_factor.unsqueeze(1).to_broadcast(shape),
                op=mybir.AluOpType.mult,
            )

        for_vector = []
        for g in range(PASSES):
            b_words = turned_bank(b_rows[g]).rearrange("p (n h) -> p n h", h=HALVES)
            nc.vector.tensor_copy(out=as_words(bt[:, now, g]), in_=b_words[:, now])
            for_vector.append(turned_bank(a_rows[g]).bitcast(BF16).rearrange("p (n t) -> p n t", t=PACK))
            if g == 0:
                multiply_first(nc.vector, 0, for_vector[0], 0, J_GROUP)
            nc.scalar.copy(out=at[:, g].rearrange("p n t -> p (n t)").bitcast(F32), in_=turned_bank(a_rows[g]))
            multiply_first(nc.gpsimd, g, at[:, g], J_FRONT - gpsimd_values, J_FRONT)
            convert_for_scalar(bt[:], slice(0, 1), min(pairs), slice(g, g + 1))
            if g == 0:
                scalar_run(0, 1)
        multiply_first(nc.vector, 0, for_vector[0], J_GROUP, front // PASSES)
        for g in range(PASSES):
            turn(b_rows[g], b_turned[:, :, g])
        scalar_run(1, 2)
        own = slice(J_FRONT - max(shares(n)[2] for n in range(1, N_STEPS)), J_FRONT)
        nc.scalar.copy(
            out=bt[:].rearrange("p (s j) g t -> p s j (g t)", j=J_STEP)[:, 1:, own].bitcast(F32),
            in_=b_turned[:].rearrange("p (s j) g h -> p s j (g h)", j=J_STEP)[:, 1:, own],
        )
        convert_for_scalar(bt_in_psum, slice(1, N_STEPS), min(scalar_pairs(n)[0] for n in range(1, N_STEPS)), slice(0, PASSES))
        multiply_first(nc.vector, 1, for_vector[1], 0, front // PASSES)
        scalar_run(2, len(pairs))

        runs = [list(range(n, n + COPIES)) for n in range(0, GROUPS, COPIES)]
        step_products, copied_sums, late = {0: tiles}, {}, []
        for step in range(1, N_STEPS):
            tiles = product_tiles()
            step_products[step] = tiles
            multiply_on_vector(step, tiles)
            multiply_on_gpsimd(step, tiles)
            for groups, copied in copied_sums.get(step - 2, []):
                subtract_copied_and_store(step - 2, groups, copied)
            pairs = scalar_pairs(step)
            scalar_run = multiply_on_scalar(step, tiles, pairs)
            scalar_run(0, SCALAR_FIRST)
            accs = quantise_and_contract(step_products[step - 1], range(GROUPS))
            if subtracts_on_gpsimd(step - 1):
                at_once = runs[:1] if step == N_STEPS - 2 else runs
                copied_sums[step - 1] = [(groups, copy_sums(accs, groups)) for groups in at_once]
                late = [(groups, accs) for groups in runs if groups not in at_once]
            else:
                subtract_and_store(step - 1, accs)
                for groups, accs in late:
                    subtract_copied_and_store(step - 2, groups, copy_sums(accs, groups))
            scalar_run(SCALAR_FIRST, len(pairs))
        last = step_products[N_STEPS - 1]
        early = quantise_and_contract(last, range(GROUPS - 1))
        subtract_and_store(N_STEPS - 1, {group: early[group] for group in range(GROUPS - 2)})
        late = quantise_and_contract(last, [GROUPS - 1], cuts=2)
        subtract_and_store(N_STEPS - 1, {GROUPS - 2: early[GROUPS - 2]})
        subtract_and_store(N_STEPS - 1, late, cuts=2)
